import numpy as np
import ml_dtypes


def mxq(x, axis, fmt="e4m3"):
    dtype, down = {"e4m3": (ml_dtypes.float8_e4m3fn, 7), "e5m2": (ml_dtypes.float8_e5m2, 14)}[fmt]
    v = np.moveaxis(np.asarray(x, np.float32).astype(ml_dtypes.bfloat16).astype(np.float64), axis, -1)
    blocks = v.reshape(v.shape[:-1] + (-1, 32))
    amax = np.abs(blocks).max(-1, keepdims=True)
    byte = np.maximum(np.where(amax > 0, np.frexp(amax)[1] - 1 + 127, 0) - down, 1)
    scale = np.exp2(byte - 127.0)
    codes = (blocks / scale).astype(np.float32).astype(dtype).astype(np.float64)
    return np.moveaxis((codes * scale).reshape(v.shape), -1, axis)


WIDE = False


def mx_kscale(k):
    if not WIDE:
        return np.ones(k)
    levels = np.array([10, -10, 5, -5, 0])
    if k % 512:
        return np.exp2(np.random.permutation(np.resize(levels, k // 32))).repeat(32)
    a = np.empty((k // 512, 16))
    for p in range(k // 512):
        a[p, :8] = np.random.permutation(np.resize(levels, 8))
        for g in range(8):
            far = levels[np.abs(levels - a[p, g]) >= 10]
            a[p, g + 8] = far[np.random.randint(len(far))]
    return np.exp2(a.ravel()).repeat(32)


BF16 = ml_dtypes.bfloat16


def bf(x):
    return np.asarray(x, np.float32).astype(BF16)


def f64(x):
    return np.asarray(x).astype(np.float64)


B, D, S, O = 1024, 512, 1024, 256
K1 = D + S
P = S // 2
EPS = 1e-6


def sigmoid(v):
    return 1.0 / (1.0 + np.exp(-v))


def setup_inputs():
    r = np.random.standard_normal
    s = np.concatenate([mx_kscale(D), np.ones(S)])
    t = mx_kscale(S)
    return {
        "inputs": bf(r((B, D)) * s[:D]),
        "states": bf(r((B, S))),
        "W1": bf(r((K1, S)) / np.sqrt(K1) / s[:, None] * t),
        "b1": bf(r(S) * 0.2 * t),
        "W2": bf(r((S, P)) / np.sqrt(S) / t[:, None]),
        "b2": bf(r(P) * 0.2),
        "excitatory_potential": bf(1.0 + 0.1 * r(S)),
        "inhibitory_potential": bf(-1.0 + 0.1 * r(S)),
        "capacitance": bf(1.0 + 0.1 * r(S)),
        "max_conductance": bf(1.0 + 0.1 * r((S, 2))),
        "mean_conductance_potential": bf(0.3 * r((S, 2))),
        "std_conductance": bf(1.0 + 0.2 * r((S, 2))),
        "gamma": bf(1.0 + 0.1 * r(S)),
        "beta": bf(0.1 * r(S)),
    }


def reference(inputs, states, W1, b1, W2, b2, excitatory_potential, inhibitory_potential, capacitance,
              max_conductance, mean_conductance_potential, std_conductance, gamma, beta):
    v = f64(states)
    b, s = v.shape
    intervals = np.ones((b, 1))
    cat = np.concatenate([f64(inputs), v], -1)
    h = (mxq(cat, 1, "e4m3") @ mxq(f64(W1), 0, "e4m3")) + f64(b1)
    pre = (mxq(h, 1, "e4m3") @ mxq(f64(W2), 0, "e4m3")) + f64(b2)
    memory_cell_inputs = np.stack([pre, -pre], -1).reshape(b, s)
    pairs = v.reshape(b, s // 2, 2)
    rolled = np.roll(pairs, 1, axis=-1)
    presyn = np.concatenate([pairs, rolled], -1).reshape(b, s, 2)
    g = f64(max_conductance) * sigmoid(f64(std_conductance) * (presyn - f64(mean_conductance_potential)))
    rev = np.stack([f64(excitatory_potential), f64(inhibitory_potential)], -1)
    diff = rev - v[..., None]
    states_change = (memory_cell_inputs + np.sum(g * diff, -1)) / f64(capacitance) * intervals
    x = v + states_change
    mu = np.mean(x, -1, keepdims=True)
    var = np.mean((x - mu) ** 2, -1, keepdims=True)
    return (x - mu) * (1.0 / np.sqrt(var + EPS)) * f64(gamma) + f64(beta)

@@ -1,0 +1,492 @@
+from contextlib import ExitStack
+
+import concourse.mybir as mybir
+from concourse.masks import make_identity
+
+F32 = mybir.dt.float32
+BF16 = mybir.dt.bfloat16
+U32 = mybir.dt.uint32
+U8 = mybir.dt.uint8
+FP8X4 = mybir.dt.float8_e4m3fn_x4
+ALU = mybir.AluOpType
+FUNC = mybir.ActivationFunctionType
+
+P = 128
+PACK = 4
+K_PASS = P * PACK
+BANK = 512
+
+ROWS, D_IN, CELLS = 1024, 512, 1024
+PAIRS = CELLS // 2
+K1 = D_IN + CELLS
+EPS = 1e-6
+
+ROW_TILES = ROWS // P
+HALF = ROWS // 2
+HALVES = 2
+TILES_PER_HALF = HALF // P
+PASSES_1 = K1 // K_PASS
+PASSES_2 = CELLS // K_PASS
+PAIR_BLOCKS = PAIRS // P
+N_COLS = 2 * PAIR_BLOCKS
+
+FLOPS = 2 * ROWS * K1 * CELLS + 2 * ROWS * CELLS * PAIRS
+
+
+def tile_memorylayercell_pa_kernel(
+    tc,
+    inputs,
+    states,
+    W1,
+    b1,
+    W2,
+    b2,
+    excitatory_potential,
+    inhibitory_potential,
+    capacitance,
+    max_conductance,
+    mean_conductance_potential,
+    std_conductance,
+    gamma,
+    beta,
+    out,
+):
+    nc = tc.nc
+    with ExitStack() as ctx:
+        consts = ctx.enter_context(tc.tile_pool(name="consts", bufs=1))
+        keep = ctx.enter_context(tc.tile_pool(name="keep", bufs=1))
+        terms = ctx.enter_context(tc.tile_pool(name="terms", bufs=1))
+        small = ctx.enter_context(tc.tile_pool(name="small", bufs=4))
+        psum = ctx.enter_context(tc.psum_pool(name="psum", bufs=8))
+
+        def new_bank(label):
+            return psum.tile([P, BANK], F32, name=label, tag="bank")
+
+        ident_f32 = consts.tile([P, P], F32)
+        make_identity(nc, ident_f32[:])
+        ident_bf16 = consts.tile([P, P], BF16)
+        make_identity(nc, ident_bf16[:])
+
+        vec_rows = consts.tile([P, 4 * P], BF16)
+        mat_rows = consts.tile([P, 8 * P], BF16)
+        bias_rows = consts.tile([P, 4 * P], BF16)
+        nc.vector.memset(vec_rows[:], 0.0)
+        nc.vector.memset(mat_rows[:], 0.0)
+        nc.vector.memset(bias_rows[:], 0.0)
+        for v, vec in enumerate((excitatory_potential, inhibitory_potential, capacitance)):
+            nc.scalar.dma_start(
+                out=vec_rows[2 * v : 2 * v + 2, :], in_=vec.rearrange("(k c) -> k c", k=2)
+            )
+        for a, mat in enumerate((max_conductance, mean_conductance_potential, std_conductance)):
+            nc.scalar.dma_start(
+                out=mat_rows[2 * a : 2 * a + 2, :],
+                in_=mat.rearrange("(k c) s -> k (c s)", k=2),
+            )
+        nc.scalar.dma_start(out=bias_rows[0:2, :], in_=b1.rearrange("(k c) -> k c", k=2))
+        nc.scalar.dma_start(out=bias_rows[2:4, 0 : 2 * P], in_=b2.rearrange("(k c) -> k c", k=2))
+
+        with (
+            tc.tile_pool(name="natural", bufs=1) as natural,
+            tc.tile_pool(name="w_raw", bufs=3) as w_raw_pool,
+            tc.tile_pool(name="w_grouped", bufs=2) as w_grouped_pool,
+        ):
+
+            states_rows = states.rearrange("(p t) s -> p t s", t=ROW_TILES)
+            inputs_rows = inputs.rearrange("(p t) s -> p t s", t=ROW_TILES)
+            out_rows = out.rearrange("(p t) s -> p t s", t=ROW_TILES)
+            states_nat = natural.tile([P, ROW_TILES, CELLS], BF16)
+            inputs_nat = natural.tile([P, ROW_TILES, D_IN], BF16)
+
+            def load_rows(h):
+                tiles = slice(TILES_PER_HALF * h, TILES_PER_HALF * (h + 1))
+                nc.sync.dma_start(out=states_nat[:, tiles, :], in_=states_rows[:, tiles, :])
+                nc.sync.dma_start(out=inputs_nat[:, tiles, :], in_=inputs_rows[:, tiles, :])
+
+            def load_w1(g):
+                raw = w_raw_pool.tile([P, PACK, CELLS], BF16, name="w1_raw", tag="w_raw")
+                nc.sync.dma_start(
+                    out=raw[:],
+                    in_=W1[K_PASS * g : K_PASS * (g + 1), :].rearrange("(q t) s -> q t s", t=PACK),
+                )
+                return raw
+
+            w1_raw = [load_w1(0)]
+            load_rows(0)
+            w1_raw.append(load_w1(1))
+            w1_raw.append(load_w1(2))
+            load_rows(1)
+            w2_raw = w_raw_pool.tile([P, PASSES_2, PACK, PAIRS], BF16, name="w2_raw", tag="w_raw")
+            nc.sync.dma_start(
+                out=w2_raw[:], in_=W2.rearrange("(g p t) n -> p g t n", g=PASSES_2, t=PACK)
+            )
+
+            vec_bank = new_bank("vec_bank")
+            mat_bank = new_bank("mat_bank")
+            vec_words = vec_rows[:].bitcast(F32)
+            mat_words = mat_rows[:].bitcast(F32)
+            for u in range(2):
+                nc.tensor.transpose(
+                    vec_bank[:, P * u : P * (u + 1)], vec_words[:, u : 2 * P : 2], ident_f32[:]
+                )
+            for q in range(4):
+                nc.tensor.transpose(
+                    mat_bank[:, P * q : P * (q + 1)], mat_words[:, q : 4 * P : 4], ident_f32[:]
+                )
+            vec_small = consts.tile([P, 2, 6], F32)
+            nc.vector.tensor_copy(
+                out=vec_small[:],
+                in_=vec_bank[:, 0 : 2 * P].rearrange("p (u r) -> p u r", u=2)[:, :, 0:6],
+            )
+            mat_small = consts.tile([P, 4, 6], F32)
+            nc.vector.tensor_copy(
+                out=mat_small[:], in_=mat_bank[:].rearrange("p (q r) -> p q r", q=4)[:, :, 0:6]
+            )
+
+            bias_bank = psum.tile([P, 6, P], BF16, name="bias_bank", tag="bank")
+            for t in range(PACK):
+                nc.tensor.transpose(
+                    bias_bank[:, t, :], bias_rows[:, t : 4 * P : 4], ident_bf16[:]
+                )
+            for u in range(2):
+                nc.tensor.transpose(
+                    bias_bank[:, 4 + u, :], bias_rows[:, u : 2 * P : 2], ident_bf16[:]
+                )
+            b1_cols = consts.tile([P, PASSES_2, PACK], F32)
+            nc.vector.tensor_copy(
+                out=b1_cols[:].rearrange("p g t -> p t g"), in_=bias_bank[:, 0:PACK, 0:2]
+            )
+            b2_cols = consts.tile([P, 2, 2], F32)
+            nc.vector.tensor_copy(
+                out=b2_cols[:].rearrange("p k u -> p u k"), in_=bias_bank[:, 4:6, 2:4]
+            )
+
+            vecs = consts.tile([P, 3, N_COLS], F32)
+            nc.vector.tensor_copy(
+                out=vecs[:].rearrange("p v (k u e) -> p (v k) u e", k=2, u=2),
+                in_=vec_small[:]
+                .rearrange("p u r -> p (u r)")
+                .bitcast(BF16)
+                .rearrange("p (u r e) -> p r u e", u=2, e=2),
+            )
+            mats = consts.tile([P, 3, N_COLS, 2], F32)
+            nc.vector.tensor_copy(
+                out=mats[:].rearrange("p a (k q) s -> p (a k) q s", k=2),
+                in_=mat_small[:]
+                .rearrange("p q r -> p (q r)")
+                .bitcast(BF16)
+                .rearrange("p (q r s) -> p r q s", q=4, s=2),
+            )
+            reversal = vecs[:, 0:2, :]
+            max_cond = mats[:, 0, :, :]
+            mean_pot = mats[:, 1, :, :]
+            slope = mats[:, 2, :, :]
+
+            inv_cap = consts.tile([P, N_COLS], F32)
+            nc.vector.reciprocal(out=inv_cap[:], in_=vecs[:, 2, :])
+            neg_gain = consts.tile([P, N_COLS, 2], F32)
+            nc.vector.scalar_tensor_tensor(
+                out=neg_gain[:],
+                in0=max_cond,
+                scalar=-1.0,
+                in1=inv_cap[:].unsqueeze(2).to_broadcast([P, N_COLS, 2]),
+                op0=ALU.mult,
+                op1=ALU.mult,
+            )
+            shift = consts.tile([P, N_COLS, 2], F32)
+            nc.vector.scalar_tensor_tensor(
+                out=shift[:], in0=slope, scalar=-1.0, in1=mean_pot, op0=ALU.mult, op1=ALU.mult
+            )
+            sign = consts.tile([P, PAIR_BLOCKS, 2], F32)
+            nc.vector.memset(sign[:, :, 0], 1.0)
+            nc.vector.memset(sign[:, :, 1], -1.0)
+            drive_gain = consts.tile([P, N_COLS], F32)
+            nc.vector.tensor_mul(
+                out=drive_gain[:], in0=inv_cap[:], in1=sign[:].rearrange("p j e -> p (j e)")
+            )
+            drive_bias = consts.tile([P, N_COLS], F32)
+            nc.vector.tensor_mul(
+                out=drive_bias[:].rearrange("p (j e) -> p j e", e=2),
+                in0=drive_gain[:].rearrange("p (j e) -> p j e", e=2),
+                in1=b2_cols[:]
+                .rearrange("p k u -> p (k u)")
+                .unsqueeze(2)
+                .to_broadcast([P, PAIR_BLOCKS, 2]),
+            )
+            nc.vector.tensor_add(out=drive_bias[:], in0=drive_bias[:], in1=vecs[:, 0, :])
+            neg_half = consts.tile([P, 1], F32)
+            nc.vector.memset(neg_half[:], -0.5)
+
+            cat_grouped = keep.tile([P, PASSES_1, ROWS, PACK], BF16, align_bytes=64)
+            cat_codes = keep.tile([P, PASSES_1, ROWS], U32, align_bytes=64)
+            cat_scales = keep.tile([P, PASSES_1, ROWS], U8, align_bytes=64)
+            cat_words = cat_grouped[:].bitcast(F32)
+            inputs_words = inputs_nat[:].bitcast(F32)
+            states_words = states_nat[:].bitcast(F32)
+
+            def transpose_cat(g, t0):
+                bank = new_bank("cat_bank")
+                for u in range(2):
+                    for i in range(2):
+                        if g == 0:
+                            words = inputs_words[:, t0 + i, u : 2 * P : 2]
+                        else:
+                            first = 2 * P * (g - 1)
+                            words = states_words[:, t0 + i, first + u : first + 2 * P : 2]
+                        nc.tensor.transpose(
+                            bank[:, P * (2 * u + i) : P * (2 * u + i + 1)], words, ident_f32[:]
+                        )
+                nc.scalar.copy(
+                    out=cat_words[:, g, P * t0 : P * (t0 + 2), :],
+                    in_=bank[:].rearrange("p (u r) -> p r u", u=2),
+                )
+
+            def quantise_cat(g, h):
+                rows = slice(HALF * h, HALF * (h + 1))
+                nc.vector.quantize_mx(
+                    out=cat_codes[:, g, rows].bitcast(FP8X4),
+                    scales=cat_scales[:, g, rows],
+                    in_=cat_grouped[:, g, rows, :].rearrange("p r t -> p (r t)"),
+                )
+
+            for h in range(HALVES):
+                for g in (1, 2, 0):
+                    for t0 in range(TILES_PER_HALF * h, TILES_PER_HALF * (h + 1), 2):
+                        transpose_cat(g, t0)
+                for g in range(PASSES_1):
+                    quantise_cat(g, h)
+
+            w1_codes = keep.tile([P, PASSES_1, CELLS], U32, align_bytes=64)
+            w1_scales = keep.tile([P, PASSES_1, CELLS], U8, align_bytes=64)
+            w2_codes = keep.tile([P, PASSES_2, PAIRS], U32, align_bytes=64)
+            w2_scales = keep.tile([P, PASSES_2, PAIRS], U8, align_bytes=64)
+
+            for g in range(PASSES_1):
+                w1_grouped = w_grouped_pool.tile(
+                    [P, CELLS, PACK], BF16, name="w1_grouped", tag="w_grouped", align_bytes=64
+                )
+                nc.vector.tensor_copy(
+                    out=w1_grouped[:].rearrange("p (g i m) t -> p g m t i", g=PASSES_2, i=PACK),
+                    in_=w1_raw[g][:].rearrange("p t (g m i) -> p g m t i", g=PASSES_2, i=PACK),
+                )
+                nc.vector.quantize_mx(
+                    out=w1_codes[:, g, :].bitcast(FP8X4),
+                    scales=w1_scales[:, g, :],
+                    in_=w1_grouped[:].rearrange("p c t -> p (c t)"),
+                )
+            w2_grouped = w_grouped_pool.tile(
+                [P, PASSES_2, PAIRS, PACK], BF16, name="w2_grouped", tag="w_grouped", align_bytes=64
+            )
+            for g in range(PASSES_2):
+                nc.vector.tensor_copy(
+                    out=w2_grouped[:, g, :, :].rearrange("p (k u m) t -> p k m t u", k=2, u=2),
+                    in_=w2_raw[:, g, :, :].rearrange("p t (k m u) -> p k m t u", k=2, u=2),
+                )
+            nc.vector.quantize_mx(
+                out=w2_codes[:].rearrange("p g c -> p (g c)").bitcast(FP8X4),
+                scales=w2_scales[:].rearrange("p g c -> p (g c)"),
+                in_=w2_grouped[:].rearrange("p g c t -> p (g c t)"),
+            )
+
+        late = ctx.enter_context(tc.tile_pool(name="late", bufs=1))
+        row_pool = ctx.enter_context(tc.tile_pool(name="row_pool", bufs=2))
+        unused_pool = ctx.enter_context(tc.tile_pool(name="unused_pool", bufs=4))
+        gamma_rows = late.tile([P, CELLS], BF16)
+        beta_rows = late.tile([P, CELLS], BF16)
+        nc.sync.dma_start(out=gamma_rows[:], in_=gamma.partition_broadcast(P))
+        nc.sync.dma_start(out=beta_rows[:], in_=beta.partition_broadcast(P))
+
+        h_grouped = keep.tile([P, PASSES_2, ROWS, PACK], BF16, align_bytes=64)
+        h_codes = keep.tile([P, PASSES_2, ROWS], U32, align_bytes=64)
+        h_scales = keep.tile([P, PASSES_2, ROWS], U8, align_bytes=64)
+
+        def first_product(g2, t):
+            rows = slice(P * t, P * (t + 1))
+            bank = new_bank("h_bank")
+            for t4 in range(PACK):
+                cols = slice(K_PASS * g2 + P * t4, K_PASS * g2 + P * (t4 + 1))
+                for g in range(PASSES_1):
+                    nc.tensor.matmul_mx(
+                        out=bank[:, P * t4 : P * (t4 + 1)],
+                        lhsT=w1_codes[:, g, cols].bitcast(FP8X4),
+                        lhsT_scale=w1_scales[:, g, cols],
+                        rhs=cat_codes[:, g, rows].bitcast(FP8X4),
+                        rhs_scale=cat_scales[:, g, rows],
+                        start=(g == 0),
+                        stop=(g == PASSES_1 - 1),
+                    )
+            nc.vector.tensor_tensor(
+                out=h_grouped[:, g2, rows, :],
+                in0=bank[:].rearrange("p (t r) -> p r t", t=PACK),
+                in1=b1_cols[:, g2, :].unsqueeze(1).to_broadcast([P, P, PACK]),
+                op=ALU.add,
+            )
+
+        def quantise_h(g2, h):
+            rows = slice(HALF * h, HALF * (h + 1))
+            nc.vector.quantize_mx(
+                out=h_codes[:, g2, rows].bitcast(FP8X4),
+                scales=h_scales[:, g2, rows],
+                in_=h_grouped[:, g2, rows, :].rearrange("p r t -> p (r t)"),
+            )
+
+        for h in range(HALVES):
+            for g2 in range(PASSES_2):
+                for t in range(TILES_PER_HALF * h, TILES_PER_HALF * (h + 1)):
+                    first_product(g2, t)
+                quantise_h(g2, h)
+
+        drive = {}
+
+        def second_product(h, jb):
+            rows = slice(HALF * h, HALF * (h + 1))
+            cols = slice(P * jb, P * (jb + 1))
+            bank = new_bank("pre_bank")
+            for g2 in range(PASSES_2):
+                nc.tensor.matmul_mx(
+                    out=bank[:],
+                    lhsT=w2_codes[:, g2, cols].bitcast(FP8X4),
+                    lhsT_scale=w2_scales[:, g2, cols],
+                    rhs=h_codes[:, g2, rows].bitcast(FP8X4),
+                    rhs_scale=h_scales[:, g2, rows],
+                    start=(g2 == 0),
+                    stop=(g2 == PASSES_2 - 1),
+                )
+            for e in range(2):
+                c = 2 * jb + e
+                drive[h, jb, e] = late.tile([P, HALF], F32, name="drive_%d_%d_%d" % (h, jb, e))
+                nc.scalar.activation(
+                    out=drive[h, jb, e][:],
+                    in_=bank[:],
+                    func=FUNC.Identity,
+                    scale=drive_gain[:, c : c + 1],
+                    bias=drive_bias[:, c : c + 1],
+                )
+
+        for h in range(HALVES):
+            for jb in range(PAIR_BLOCKS):
+                second_product(h, jb)
+
+        self_term = {}
+        partner_term = {}
+
+        def currents(h, jb, e):
+            rows = slice(HALF * h, HALF * (h + 1))
+            c = 2 * jb + e
+            g, u = 1 + jb // 2, jb % 2
+            v_own = cat_grouped[:, g, rows, 2 * u + e]
+            v_partner = cat_grouped[:, g, rows, 2 * u + 1 - e]
+            own = terms.tile([P, HALF], F32, name="self_%d_%d_%d" % (h, jb, e))
+            other = terms.tile([P, HALF], F32, name="partner_%d_%d_%d" % (h, jb, e))
+            for syn, (dst, v_pre) in enumerate(((own, v_own), (other, v_partner))):
+                nc.scalar.activation(
+                    out=dst[:],
+                    in_=v_pre,
+                    func=FUNC.Sigmoid,
+                    scale=slope[:, c : c + 1, syn],
+                    bias=shift[:, c : c + 1, syn],
+                )
+            nc.scalar.activation(
+                out=own[:], in_=own[:], func=FUNC.Identity, scale=neg_gain[:, c : c + 1, 0], bias=1.0
+            )
+            nc.vector.tensor_scalar_mul(out=other[:], in0=other[:], scalar1=neg_gain[:, c : c + 1, 1])
+            for syn, dst in enumerate((own, other)):
+                nc.vector.scalar_tensor_tensor(
+                    out=dst[:],
+                    in0=v_own,
+                    scalar=reversal[:, syn, c : c + 1],
+                    in1=dst[:],
+                    op0=ALU.subtract,
+                    op1=ALU.mult,
+                )
+            self_term[h, jb, e] = own
+            partner_term[h, jb, e] = other
+
+        for h in range(HALVES):
+            for jb in range(PAIR_BLOCKS):
+                for e in range(2):
+                    currents(h, jb, e)
+
+        def finish_rows(t):
+            h, lanes = t // TILES_PER_HALF, slice(P * (t % TILES_PER_HALF), P * (t % TILES_PER_HALF + 1))
+            neg_mean_parts = small.tile([P, 2], F32, name="neg_mean_parts")
+            x_banks = []
+            for k in range(2):
+                bank = new_bank("x_bank")
+                for e in range(2):
+                    for jl in range(2):
+                        jb = 2 * k + jl
+                        block = slice(P * (2 * jl + e), P * (2 * jl + e + 1))
+                        parts = (self_term[h, jb, e], partner_term[h, jb, e], drive[h, jb, e])
+                        for i, part in enumerate(parts):
+                            nc.tensor.matmul(
+                                out=bank[:, block],
+                                lhsT=part[:, lanes],
+                                rhs=ident_f32[:],
+                                is_transpose=True,
+                                start=(i == 0),
+                                stop=(i == len(parts) - 1),
+                            )
+                unused = unused_pool.tile([P, BANK], BF16, name="unused")
+                nc.scalar.activation(
+                    out=unused[:],
+                    in_=bank[:],
+                    func=FUNC.Identity,
+                    scale=-1.0 / CELLS,
+                    accum_out=neg_mean_parts[:, k : k + 1],
+                )
+                x_banks.append(bank)
+            neg_mean = small.tile([P, 1], F32, name="neg_mean")
+            nc.scalar.activation(
+                out=neg_mean[:],
+                in_=neg_mean_parts[:, 0:1],
+                func=FUNC.Identity,
+                bias=neg_mean_parts[:, 1:2],
+            )
+            square_parts = small.tile([P, 2], F32, name="square_parts")
+            for k in range(2):
+                unused = unused_pool.tile([P, BANK], BF16, name="unused")
+                nc.scalar.activation(
+                    out=unused[:],
+                    in_=x_banks[k][:],
+                    func=FUNC.Square,
+                    bias=neg_mean[:, 0:1],
+                    accum_out=square_parts[:, k : k + 1],
+                )
+            part_eps = small.tile([P, 1], F32, name="part_eps")
+            nc.scalar.activation(
+                out=part_eps[:], in_=square_parts[:, 1:2], func=FUNC.Identity, scale=1.0 / CELLS, bias=EPS
+            )
+            var_eps = small.tile([P, 1], F32, name="var_eps")
+            nc.scalar.activation(
+                out=var_eps[:],
+                in_=square_parts[:, 0:1],
+                func=FUNC.Identity,
+                scale=1.0 / CELLS,
+                bias=part_eps[:, 0:1],
+            )
+            rstd = small.tile([P, 1], F32, name="rstd")
+            nc.gpsimd.tensor_tensor(out=rstd[:], in0=var_eps[:], in1=neg_half[:], op=ALU.pow)
+            centred = row_pool.tile([P, CELLS], F32, name="centred")
+            for k in range(2):
+                cells = slice(BANK * k, BANK * (k + 1))
+                nc.vector.scalar_tensor_tensor(
+                    out=centred[:, cells].rearrange("p (m b) -> p m b", b=4),
+                    in0=x_banks[k][:].rearrange("p (b m) -> p m b", b=4),
+                    scalar=neg_mean[:, 0:1],
+                    in1=gamma_rows[:, cells].rearrange("p (m b) -> p m b", b=4),
+                    op0=ALU.add,
+                    op1=ALU.mult,
+                )
+            result = row_pool.tile([P, CELLS], F32, name="result")
+            nc.vector.scalar_tensor_tensor(
+                out=result[:],
+                in0=centred[:],
+                scalar=rstd[:, 0:1],
+                in1=beta_rows[:],
+                op0=ALU.mult,
+                op1=ALU.add,
+            )
+            nc.sync.dma_start(out=out_rows[:, t, :], in_=result[:])
+
+        for t in range(ROW_TILES):
+            finish_rows(t)

@@ -54,6 +54,8 @@ def tile_memorylayercell_pa_kernel(
     nc = tc.nc
     with ExitStack() as ctx:
         consts = ctx.enter_context(tc.tile_pool(name="consts", bufs=1))
+        gamma_rows = consts.tile([P, CELLS], BF16)
+        beta_rows = consts.tile([P, CELLS], BF16)
         keep = ctx.enter_context(tc.tile_pool(name="keep", bufs=1))
         terms = ctx.enter_context(tc.tile_pool(name="terms", bufs=1))
         small = ctx.enter_context(tc.tile_pool(name="small", bufs=4))
@@ -62,32 +64,26 @@ def tile_memorylayercell_pa_kernel(
         def new_bank(label):
             return psum.tile([P, BANK], F32, name=label, tag="bank")
 
-        ident_f32 = consts.tile([P, P], F32)
-        make_identity(nc, ident_f32[:])
-        ident_bf16 = consts.tile([P, P], BF16)
-        make_identity(nc, ident_bf16[:])
 
-        vec_rows = consts.tile([P, 4 * P], BF16)
-        mat_rows = consts.tile([P, 8 * P], BF16)
-        bias_rows = consts.tile([P, 4 * P], BF16)
-        nc.vector.memset(vec_rows[:], 0.0)
-        nc.vector.memset(mat_rows[:], 0.0)
-        nc.vector.memset(bias_rows[:], 0.0)
-        for v, vec in enumerate((excitatory_potential, inhibitory_potential, capacitance)):
+        first_rows = consts.tile([P, 8 * P], BF16)
+        later_rows = consts.tile([P, 8 * P], BF16)
+        nc.gpsimd.memset(first_rows[:].bitcast(F32), 0.0)
+        for a, mat in enumerate((mean_conductance_potential, std_conductance)):
             nc.scalar.dma_start(
-                out=vec_rows[2 * v : 2 * v + 2, :], in_=vec.rearrange("(k c) -> k c", k=2)
-            )
-        for a, mat in enumerate((max_conductance, mean_conductance_potential, std_conductance)):
-            nc.scalar.dma_start(
-                out=mat_rows[2 * a : 2 * a + 2, :],
+                out=first_rows[2 * a : 2 * a + 2, :],
                 in_=mat.rearrange("(k c) s -> k (c s)", k=2),
             )
-        nc.scalar.dma_start(out=bias_rows[0:2, :], in_=b1.rearrange("(k c) -> k c", k=2))
-        nc.scalar.dma_start(out=bias_rows[2:4, 0 : 2 * P], in_=b2.rearrange("(k c) -> k c", k=2))
+
+        table_probe = consts.tile([P, 1], F32)
+        nc.vector.memset(table_probe[:], 0.0)
+        nc.scalar.activation(out=table_probe[:], in_=table_probe[:], func=FUNC.Sigmoid)
+        ident_f32 = consts.tile([P, P], F32)
+        make_identity(nc, ident_f32[:])
+        nc.gpsimd.memset(later_rows[:].bitcast(F32), 0.0)
 
         with (
             tc.tile_pool(name="natural", bufs=1) as natural,
-            tc.tile_pool(name="w_raw", bufs=3) as w_raw_pool,
+            tc.tile_pool(name="w_raw", bufs=1) as w_raw_pool,
             tc.tile_pool(name="w_grouped", bufs=2) as w_grouped_pool,
         ):
 
@@ -97,124 +93,52 @@ def tile_memorylayercell_pa_kernel(
             states_nat = natural.tile([P, ROW_TILES, CELLS], BF16)
             inputs_nat = natural.tile([P, ROW_TILES, D_IN], BF16)
 
-            def load_rows(h):
-                tiles = slice(TILES_PER_HALF * h, TILES_PER_HALF * (h + 1))
+            def load_states(t0, n):
+                tiles = slice(t0, t0 + n)
                 nc.sync.dma_start(out=states_nat[:, tiles, :], in_=states_rows[:, tiles, :])
+
+            def load_inputs(t0, n):
+                tiles = slice(t0, t0 + n)
                 nc.sync.dma_start(out=inputs_nat[:, tiles, :], in_=inputs_rows[:, tiles, :])
 
-            def load_w1(g):
-                raw = w_raw_pool.tile([P, PACK, CELLS], BF16, name="w1_raw", tag="w_raw")
+            def load_w1(g, first, width):
+                cols = slice(first, first + width)
+                raw = w_raw_pool.tile([P, PACK, width], BF16, name="w1_raw_%d_%d" % (g, first))
                 nc.sync.dma_start(
                     out=raw[:],
-                    in_=W1[K_PASS * g : K_PASS * (g + 1), :].rearrange("(q t) s -> q t s", t=PACK),
+                    in_=W1[K_PASS * g : K_PASS * (g + 1), cols].rearrange("(q t) s -> q t s", t=PACK),
                 )
-                return raw
+                for g2 in range(first // K_PASS, (first + width) // K_PASS):
+                    w1_raw[g, g2] = raw[:, :, K_PASS * g2 - first : K_PASS * (g2 + 1) - first]
 
-            w1_raw = [load_w1(0)]
-            load_rows(0)
-            w1_raw.append(load_w1(1))
-            w1_raw.append(load_w1(2))
-            load_rows(1)
-            w2_raw = w_raw_pool.tile([P, PASSES_2, PACK, PAIRS], BF16, name="w2_raw", tag="w_raw")
+            w1_raw = {}
+            w2_raw = w_raw_pool.tile([P, PASSES_2, PACK, PAIRS], BF16, name="w2_raw")
+            load_w1(0, 0, K_PASS)
+            load_states(0, 2)
+            load_w1(0, K_PASS, K_PASS)
+            load_states(2, 2)
+            load_w1(1, 0, K_PASS)
+            load_inputs(0, TILES_PER_HALF)
+            load_w1(1, K_PASS, K_PASS)
+            load_w1(2, 0, CELLS)
+            nc.sync.dma_start(
+                out=later_rows[0:2, :], in_=max_conductance.rearrange("(k c) s -> k (c s)", k=2)
+            )
+            for v, vec in enumerate((excitatory_potential, inhibitory_potential, capacitance, b1)):
+                nc.sync.dma_start(
+                    out=later_rows[2 + 2 * v : 4 + 2 * v, 0 : 4 * P],
+                    in_=vec.rearrange("(k c) -> k c", k=2),
+                )
+            nc.sync.dma_start(
+                out=later_rows[10:12, 0 : 2 * P], in_=b2.rearrange("(k c) -> k c", k=2)
+            )
+            load_states(TILES_PER_HALF, TILES_PER_HALF)
             nc.sync.dma_start(
                 out=w2_raw[:], in_=W2.rearrange("(g p t) n -> p g t n", g=PASSES_2, t=PACK)
             )
-
-            vec_bank = new_bank("vec_bank")
-            mat_bank = new_bank("mat_bank")
-            vec_words = vec_rows[:].bitcast(F32)
-            mat_words = mat_rows[:].bitcast(F32)
-            for u in range(2):
-                nc.tensor.transpose(
-                    vec_bank[:, P * u : P * (u + 1)], vec_words[:, u : 2 * P : 2], ident_f32[:]
-                )
-            for q in range(4):
-                nc.tensor.transpose(
-                    mat_bank[:, P * q : P * (q + 1)], mat_words[:, q : 4 * P : 4], ident_f32[:]
-                )
-            vec_small = consts.tile([P, 2, 6], F32)
-            nc.vector.tensor_copy(
-                out=vec_small[:],
-                in_=vec_bank[:, 0 : 2 * P].rearrange("p (u r) -> p u r", u=2)[:, :, 0:6],
-            )
-            mat_small = consts.tile([P, 4, 6], F32)
-            nc.vector.tensor_copy(
-                out=mat_small[:], in_=mat_bank[:].rearrange("p (q r) -> p q r", q=4)[:, :, 0:6]
-            )
-
-            bias_bank = psum.tile([P, 6, P], BF16, name="bias_bank", tag="bank")
-            for t in range(PACK):
-                nc.tensor.transpose(
-                    bias_bank[:, t, :], bias_rows[:, t : 4 * P : 4], ident_bf16[:]
-                )
-            for u in range(2):
-                nc.tensor.transpose(
-                    bias_bank[:, 4 + u, :], bias_rows[:, u : 2 * P : 2], ident_bf16[:]
-                )
-            b1_cols = consts.tile([P, PASSES_2, PACK], F32)
-            nc.vector.tensor_copy(
-                out=b1_cols[:].rearrange("p g t -> p t g"), in_=bias_bank[:, 0:PACK, 0:2]
-            )
-            b2_cols = consts.tile([P, 2, 2], F32)
-            nc.vector.tensor_copy(
-                out=b2_cols[:].rearrange("p k u -> p u k"), in_=bias_bank[:, 4:6, 2:4]
-            )
-
-            vecs = consts.tile([P, 3, N_COLS], F32)
-            nc.vector.tensor_copy(
-                out=vecs[:].rearrange("p v (k u e) -> p (v k) u e", k=2, u=2),
-                in_=vec_small[:]
-                .rearrange("p u r -> p (u r)")
-                .bitcast(BF16)
-                .rearrange("p (u r e) -> p r u e", u=2, e=2),
-            )
-            mats = consts.tile([P, 3, N_COLS, 2], F32)
-            nc.vector.tensor_copy(
-                out=mats[:].rearrange("p a (k q) s -> p (a k) q s", k=2),
-                in_=mat_small[:]
-                .rearrange("p q r -> p (q r)")
-                .bitcast(BF16)
-                .rearrange("p (q r s) -> p r q s", q=4, s=2),
-            )
-            reversal = vecs[:, 0:2, :]
-            max_cond = mats[:, 0, :, :]
-            mean_pot = mats[:, 1, :, :]
-            slope = mats[:, 2, :, :]
-
-            inv_cap = consts.tile([P, N_COLS], F32)
-            nc.vector.reciprocal(out=inv_cap[:], in_=vecs[:, 2, :])
-            neg_gain = consts.tile([P, N_COLS, 2], F32)
-            nc.vector.scalar_tensor_tensor(
-                out=neg_gain[:],
-                in0=max_cond,
-                scalar=-1.0,
-                in1=inv_cap[:].unsqueeze(2).to_broadcast([P, N_COLS, 2]),
-                op0=ALU.mult,
-                op1=ALU.mult,
-            )
-            shift = consts.tile([P, N_COLS, 2], F32)
-            nc.vector.scalar_tensor_tensor(
-                out=shift[:], in0=slope, scalar=-1.0, in1=mean_pot, op0=ALU.mult, op1=ALU.mult
-            )
-            sign = consts.tile([P, PAIR_BLOCKS, 2], F32)
-            nc.vector.memset(sign[:, :, 0], 1.0)
-            nc.vector.memset(sign[:, :, 1], -1.0)
-            drive_gain = consts.tile([P, N_COLS], F32)
-            nc.vector.tensor_mul(
-                out=drive_gain[:], in0=inv_cap[:], in1=sign[:].rearrange("p j e -> p (j e)")
-            )
-            drive_bias = consts.tile([P, N_COLS], F32)
-            nc.vector.tensor_mul(
-                out=drive_bias[:].rearrange("p (j e) -> p j e", e=2),
-                in0=drive_gain[:].rearrange("p (j e) -> p j e", e=2),
-                in1=b2_cols[:]
-                .rearrange("p k u -> p (k u)")
-                .unsqueeze(2)
-                .to_broadcast([P, PAIR_BLOCKS, 2]),
-            )
-            nc.vector.tensor_add(out=drive_bias[:], in0=drive_bias[:], in1=vecs[:, 0, :])
-            neg_half = consts.tile([P, 1], F32)
-            nc.vector.memset(neg_half[:], -0.5)
+            load_inputs(TILES_PER_HALF, TILES_PER_HALF)
+            nc.sync.dma_start(out=gamma_rows[:], in_=gamma.partition_broadcast(P))
+            nc.sync.dma_start(out=beta_rows[:], in_=beta.partition_broadcast(P))
 
             cat_grouped = keep.tile([P, PASSES_1, ROWS, PACK], BF16, align_bytes=64)
             cat_codes = keep.tile([P, PASSES_1, ROWS], U32, align_bytes=64)
@@ -248,92 +172,259 @@ def tile_memorylayercell_pa_kernel(
                     in_=cat_grouped[:, g, rows, :].rearrange("p r t -> p (r t)"),
                 )
 
-            for h in range(HALVES):
-                for g in (1, 2, 0):
-                    for t0 in range(TILES_PER_HALF * h, TILES_PER_HALF * (h + 1), 2):
-                        transpose_cat(g, t0)
-                for g in range(PASSES_1):
-                    quantise_cat(g, h)
+            for g in (1, 2):
+                transpose_cat(g, 0)
+
+            def transpose_cells(bank, rows):
+                for q in range(4):
+                    nc.tensor.transpose(
+                        bank[:, P * q : P * (q + 1)], rows[:, q : 4 * P : 4], ident_f32[:]
+                    )
+
+            def widen_cells(name, bank, arrays):
+                taken = consts.tile([P, 4, 2 * arrays], F32, name=name + "_words")
+                nc.vector.tensor_copy(
+                    out=taken[:],
+                    in_=bank[:].rearrange("p (q r) -> p q r", q=4)[:, :, 0 : 2 * arrays],
+                )
+                wide = consts.tile([P, arrays, N_COLS, 2], F32, name=name)
+                nc.gpsimd.tensor_copy(
+                    out=wide[:].rearrange("p a (k q) s -> p (a k) q s", k=2),
+                    in_=taken[:]
+                    .rearrange("p q r -> p (q r)")
+                    .bitcast(BF16)
+                    .rearrange("p (q r s) -> p r q s", q=4, s=2),
+                )
+                return wide
+
+            first_bank = new_bank("first_bank")
+            transpose_cells(first_bank, first_rows[:].bitcast(F32))
+            first_cells = widen_cells("first_cells", first_bank, 2)
+            mean_pot = first_cells[:, 0, :, :]
+            slope = first_cells[:, 1, :, :]
+            shift = consts.tile([P, N_COLS, 2], F32)
+            nc.gpsimd.tensor_scalar(
+                out=shift[:], in0=mean_pot, scalar1=-1.0, scalar2=1.0, op0=ALU.mult, op1=ALU.mult
+            )
+            nc.gpsimd.tensor_tensor(out=shift[:], in0=shift[:], in1=slope, op=ALU.mult)
 
             w1_codes = keep.tile([P, PASSES_1, CELLS], U32, align_bytes=64)
             w1_scales = keep.tile([P, PASSES_1, CELLS], U8, align_bytes=64)
             w2_codes = keep.tile([P, PASSES_2, PAIRS], U32, align_bytes=64)
             w2_scales = keep.tile([P, PASSES_2, PAIRS], U8, align_bytes=64)
 
+            def regroup_w1(g, g2):
+                cols = slice(K_PASS * g2, K_PASS * (g2 + 1))
+                nc.vector.tensor_copy(
+                    out=w1_grouped[g][:, cols, :].rearrange("p (i m) t -> p m t i", i=PACK),
+                    in_=w1_raw[g, g2].rearrange("p t (m i) -> p m t i", i=PACK),
+                )
+
+            def quantise_w1(g, g2):
+                cols = slice(K_PASS * g2, K_PASS * (g2 + 1))
+                nc.vector.quantize_mx(
+                    out=w1_codes[:, g, cols].bitcast(FP8X4),
+                    scales=w1_scales[:, g, cols],
+                    in_=w1_grouped[g][:, cols, :].rearrange("p c t -> p (c t)"),
+                )
+
+            w1_grouped = []
             for g in range(PASSES_1):
-                w1_grouped = w_grouped_pool.tile(
+                grouped = w_grouped_pool.tile(
                     [P, CELLS, PACK], BF16, name="w1_grouped", tag="w_grouped", align_bytes=64
                 )
-                nc.vector.tensor_copy(
-                    out=w1_grouped[:].rearrange("p (g i m) t -> p g m t i", g=PASSES_2, i=PACK),
-                    in_=w1_raw[g][:].rearrange("p t (g m i) -> p g m t i", g=PASSES_2, i=PACK),
+                w1_grouped.append(grouped)
+
+            def quantise_w2():
+                w2_grouped = w_grouped_pool.tile(
+                    [P, PASSES_2, PAIRS, PACK], BF16, name="w2_grouped", tag="w_grouped", align_bytes=64
                 )
+                for g in range(PASSES_2):
+                    nc.vector.tensor_copy(
+                        out=w2_grouped[:, g, :, :].rearrange("p (k u m) t -> p k m t u", k=2, u=2),
+                        in_=w2_raw[:, g, :, :].rearrange("p t (k m u) -> p k m t u", k=2, u=2),
+                    )
                 nc.vector.quantize_mx(
-                    out=w1_codes[:, g, :].bitcast(FP8X4),
-                    scales=w1_scales[:, g, :],
-                    in_=w1_grouped[:].rearrange("p c t -> p (c t)"),
+                    out=w2_codes[:].rearrange("p g c -> p (g c)").bitcast(FP8X4),
+                    scales=w2_scales[:].rearrange("p g c -> p (g c)"),
+                    in_=w2_grouped[:].rearrange("p g c t -> p (g c t)"),
                 )
-            w2_grouped = w_grouped_pool.tile(
-                [P, PASSES_2, PAIRS, PACK], BF16, name="w2_grouped", tag="w_grouped", align_bytes=64
-            )
-            for g in range(PASSES_2):
-                nc.vector.tensor_copy(
-                    out=w2_grouped[:, g, :, :].rearrange("p (k u m) t -> p k m t u", k=2, u=2),
-                    in_=w2_raw[:, g, :, :].rearrange("p t (k m u) -> p k m t u", k=2, u=2),
+
+            h_grouped = keep.tile([P, PASSES_2, ROWS, PACK], BF16, align_bytes=64)
+            h_codes = keep.tile([P, PASSES_2, ROWS], U32, align_bytes=64)
+            h_scales = keep.tile([P, PASSES_2, ROWS], U8, align_bytes=64)
+
+            h_banks = {}
+
+            def first_product(g2, t):
+                rows = slice(P * t, P * (t + 1))
+                bank = new_bank("h_bank")
+                for t4 in range(PACK):
+                    cols = slice(K_PASS * g2 + P * t4, K_PASS * g2 + P * (t4 + 1))
+                    for g in range(PASSES_1):
+                        nc.tensor.matmul_mx(
+                            out=bank[:, P * t4 : P * (t4 + 1)],
+                            lhsT=w1_codes[:, g, cols].bitcast(FP8X4),
+                            lhsT_scale=w1_scales[:, g, cols],
+                            rhs=cat_codes[:, g, rows].bitcast(FP8X4),
+                            rhs_scale=cat_scales[:, g, rows],
+                            start=(g == 0),
+                            stop=(g == PASSES_1 - 1),
+                        )
+                h_banks[g2, t] = bank
+
+            def add_b1(g2, t):
+                rows = slice(P * t, P * (t + 1))
+                bank = h_banks[g2, t]
+                nc.vector.tensor_tensor(
+                    out=h_grouped[:, g2, rows, :],
+                    in0=bank[:].rearrange("p (t r) -> p r t", t=PACK),
+                    in1=b1_cols[:, g2, :].unsqueeze(1).to_broadcast([P, P, PACK]),
+                    op=ALU.add,
                 )
-            nc.vector.quantize_mx(
-                out=w2_codes[:].rearrange("p g c -> p (g c)").bitcast(FP8X4),
-                scales=w2_scales[:].rearrange("p g c -> p (g c)"),
-                in_=w2_grouped[:].rearrange("p g c t -> p (g c t)"),
+
+            def quantise_h(g2, h):
+                rows = slice(HALF * h, HALF * (h + 1))
+                nc.vector.quantize_mx(
+                    out=h_codes[:, g2, rows].bitcast(FP8X4),
+                    scales=h_scales[:, g2, rows],
+                    in_=h_grouped[:, g2, rows, :].rearrange("p r t -> p (r t)"),
+                )
+
+            terms_of = {}
+
+            def sigmoids(pool, h, c):
+                rows = slice(HALF * h, HALF * (h + 1))
+                g, b = 1 + c // PACK, c % PACK
+                own = pool.tile([P, HALF], F32, name="self_%d_%d" % (h, c))
+                other = pool.tile([P, HALF], F32, name="partner_%d_%d" % (h, c))
+                partner = b + 1 - 2 * (b % 2)
+                for syn, dst, value in ((1, other, partner), (0, own, b)):
+                    nc.scalar.activation(
+                        out=dst[:],
+                        in_=cat_grouped[:, g, rows, value],
+                        func=FUNC.Sigmoid,
+                        scale=slope[:, c : c + 1, syn],
+                        bias=shift[:, c : c + 1, syn],
+                    )
+                terms_of[h, c] = (own, other)
+
+            def self_gain(h, c):
+                own = terms_of[h, c][0]
+                nc.scalar.activation(
+                    out=own[:], in_=own[:], func=FUNC.Identity, scale=neg_gain[:, c : c + 1, 0], bias=1.0
+                )
+
+            def partner_gain(h, c):
+                other = terms_of[h, c][1]
+                nc.vector.tensor_scalar_mul(
+                    out=other[:], in0=other[:], scalar1=neg_gain[:, c : c + 1, 1]
+                )
+
+            def product(h, c, syn):
+                dst = terms_of[h, c][syn]
+                rows = slice(HALF * h, HALF * (h + 1))
+                nc.vector.scalar_tensor_tensor(
+                    out=dst[:],
+                    in0=cat_grouped[:, 1 + c // PACK, rows, c % PACK],
+                    scalar=reversal[:, syn, c : c + 1],
+                    in1=dst[:],
+                    op0=ALU.subtract,
+                    op1=ALU.mult,
+                )
+
+            for g in (1, 2):
+                transpose_cat(g, 2)
+            for t0 in (0, 2):
+                transpose_cat(0, t0)
+            for g in range(PASSES_1):
+                for g2 in range(PASSES_2):
+                    regroup_w1(g, g2)
+                for g2 in range(PASSES_2):
+                    quantise_w1(g, g2)
+                if g == 0:
+                    for g_cat in (1, 2, 0):
+                        quantise_cat(g_cat, 0)
+            later_words = later_rows[:].bitcast(F32)
+            gain_bank = new_bank("gain_bank")
+            transpose_cells(gain_bank, later_words)
+            vec_bank = new_bank("vec_bank")
+            for u in range(2):
+                nc.tensor.transpose(
+                    vec_bank[:, P * u : P * (u + 1)], later_words[:, u : 2 * P : 2], ident_f32[:]
+                )
+            nc.tensor.transpose(vec_bank[:, 2 * P : 3 * P], later_words[:, 0:P], ident_f32[:])
+            max_cond = widen_cells("max_cond", gain_bank, 1)[:, 0, :, :]
+            vec_small = consts.tile([P, 3, 10], F32)
+            nc.vector.tensor_copy(
+                out=vec_small[:],
+                in_=vec_bank[:, 0 : 3 * P].rearrange("p (u r) -> p u r", u=3)[:, :, 2:12],
             )
+            vec_halves = (
+                vec_small[:]
+                .rearrange("p u r -> p (u r)")
+                .bitcast(BF16)
+                .rearrange("p (u r e) -> p r u e", u=3, e=2)
+            )
+            vecs = consts.tile([P, 4, N_COLS], F32)
+            nc.gpsimd.tensor_copy(
+                out=vecs[:].rearrange("p v (k u e) -> p (v k) u e", k=2, u=2),
+                in_=vec_halves[:, 0:8, 0:2, :],
+            )
+            b2_cols = consts.tile([P, PAIR_BLOCKS], F32)
+            nc.gpsimd.tensor_copy(
+                out=b2_cols[:].rearrange("p (k u) -> p k u", k=2), in_=vec_halves[:, 8:10, 2, :]
+            )
+            reversal = vecs[:, 0:2, :]
+            b1_cols = vecs[:, 3, :].rearrange("p (g t) -> p g t", g=PASSES_2)
+            inv_cap = consts.tile([P, N_COLS], F32)
+            nc.vector.reciprocal(out=inv_cap[:], in_=vecs[:, 2, :])
+            neg_inv = consts.tile([P, N_COLS], F32)
+            nc.gpsimd.tensor_scalar(
+                out=neg_inv[:], in0=inv_cap[:], scalar1=-1.0, scalar2=1.0, op0=ALU.mult, op1=ALU.mult
+            )
+            neg_gain = consts.tile([P, N_COLS, 2], F32)
+            nc.gpsimd.tensor_tensor(
+                out=neg_gain[:],
+                in0=max_cond,
+                in1=neg_inv[:].unsqueeze(2).to_broadcast([P, N_COLS, 2]),
+                op=ALU.mult,
+            )
+            drive_gain = consts.tile([P, N_COLS], F32)
+            nc.gpsimd.tensor_copy(out=drive_gain[:, 0:N_COLS:2], in_=inv_cap[:, 0:N_COLS:2])
+            nc.gpsimd.tensor_copy(out=drive_gain[:, 1:N_COLS:2], in_=neg_inv[:, 1:N_COLS:2])
+            drive_bias = consts.tile([P, N_COLS], F32)
+            nc.gpsimd.tensor_tensor(
+                out=drive_bias[:].rearrange("p (j e) -> p j e", e=2),
+                in0=drive_gain[:].rearrange("p (j e) -> p j e", e=2),
+                in1=b2_cols[:].unsqueeze(2).to_broadcast([P, PAIR_BLOCKS, 2]),
+                op=ALU.mult,
+            )
+            nc.gpsimd.tensor_tensor(
+                out=drive_bias[:], in0=drive_bias[:], in1=vecs[:, 0, :], op=ALU.add
+            )
+            neg_half = consts.tile([P, 1], F32)
+            nc.gpsimd.memset(neg_half[:], -0.5)
+
+            for g in (1, 2, 0):
+                for t0 in range(TILES_PER_HALF, ROW_TILES, 2):
+                    transpose_cat(g, t0)
+            for c in range(0, N_COLS, 2):
+                sigmoids(terms, 0, c)
+                sigmoids(terms, 0, c + 1)
+                self_gain(0, c)
+                self_gain(0, c + 1)
+
+            for g2 in range(PASSES_2):
+                for t in range(TILES_PER_HALF):
+                    first_product(g2, t)
+                    add_b1(g2, t)
+                quantise_h(g2, 0)
+            quantise_w2()
 
         late = ctx.enter_context(tc.tile_pool(name="late", bufs=1))
         row_pool = ctx.enter_context(tc.tile_pool(name="row_pool", bufs=2))
         unused_pool = ctx.enter_context(tc.tile_pool(name="unused_pool", bufs=4))
-        gamma_rows = late.tile([P, CELLS], BF16)
-        beta_rows = late.tile([P, CELLS], BF16)
-        nc.sync.dma_start(out=gamma_rows[:], in_=gamma.partition_broadcast(P))
-        nc.sync.dma_start(out=beta_rows[:], in_=beta.partition_broadcast(P))
-
-        h_grouped = keep.tile([P, PASSES_2, ROWS, PACK], BF16, align_bytes=64)
-        h_codes = keep.tile([P, PASSES_2, ROWS], U32, align_bytes=64)
-        h_scales = keep.tile([P, PASSES_2, ROWS], U8, align_bytes=64)
-
-        def first_product(g2, t):
-            rows = slice(P * t, P * (t + 1))
-            bank = new_bank("h_bank")
-            for t4 in range(PACK):
-                cols = slice(K_PASS * g2 + P * t4, K_PASS * g2 + P * (t4 + 1))
-                for g in range(PASSES_1):
-                    nc.tensor.matmul_mx(
-                        out=bank[:, P * t4 : P * (t4 + 1)],
-                        lhsT=w1_codes[:, g, cols].bitcast(FP8X4),
-                        lhsT_scale=w1_scales[:, g, cols],
-                        rhs=cat_codes[:, g, rows].bitcast(FP8X4),
-                        rhs_scale=cat_scales[:, g, rows],
-                        start=(g == 0),
-                        stop=(g == PASSES_1 - 1),
-                    )
-            nc.vector.tensor_tensor(
-                out=h_grouped[:, g2, rows, :],
-                in0=bank[:].rearrange("p (t r) -> p r t", t=PACK),
-                in1=b1_cols[:, g2, :].unsqueeze(1).to_broadcast([P, P, PACK]),
-                op=ALU.add,
-            )
-
-        def quantise_h(g2, h):
-            rows = slice(HALF * h, HALF * (h + 1))
-            nc.vector.quantize_mx(
-                out=h_codes[:, g2, rows].bitcast(FP8X4),
-                scales=h_scales[:, g2, rows],
-                in_=h_grouped[:, g2, rows, :].rearrange("p r t -> p (r t)"),
-            )
-
-        for h in range(HALVES):
-            for g2 in range(PASSES_2):
-                for t in range(TILES_PER_HALF * h, TILES_PER_HALF * (h + 1)):
-                    first_product(g2, t)
-                quantise_h(g2, h)
 
         drive = {}
 
@@ -353,103 +444,63 @@ def tile_memorylayercell_pa_kernel(
                 )
             for e in range(2):
                 c = 2 * jb + e
-                drive[h, jb, e] = late.tile([P, HALF], F32, name="drive_%d_%d_%d" % (h, jb, e))
+                drive[h, c] = late.tile([P, HALF], F32, name="drive_%d_%d" % (h, c))
                 nc.scalar.activation(
-                    out=drive[h, jb, e][:],
+                    out=drive[h, c][:],
                     in_=bank[:],
                     func=FUNC.Identity,
                     scale=drive_gain[:, c : c + 1],
                     bias=drive_bias[:, c : c + 1],
                 )
 
-        for h in range(HALVES):
-            for jb in range(PAIR_BLOCKS):
-                second_product(h, jb)
+        x_banks, neg_mean, rstd, centred = {}, {}, {}, {}
 
-        self_term = {}
-        partner_term = {}
-
-        def currents(h, jb, e):
-            rows = slice(HALF * h, HALF * (h + 1))
-            c = 2 * jb + e
-            g, u = 1 + jb // 2, jb % 2
-            v_own = cat_grouped[:, g, rows, 2 * u + e]
-            v_partner = cat_grouped[:, g, rows, 2 * u + 1 - e]
-            own = terms.tile([P, HALF], F32, name="self_%d_%d_%d" % (h, jb, e))
-            other = terms.tile([P, HALF], F32, name="partner_%d_%d_%d" % (h, jb, e))
-            for syn, (dst, v_pre) in enumerate(((own, v_own), (other, v_partner))):
-                nc.scalar.activation(
-                    out=dst[:],
-                    in_=v_pre,
-                    func=FUNC.Sigmoid,
-                    scale=slope[:, c : c + 1, syn],
-                    bias=shift[:, c : c + 1, syn],
-                )
-            nc.scalar.activation(
-                out=own[:], in_=own[:], func=FUNC.Identity, scale=neg_gain[:, c : c + 1, 0], bias=1.0
-            )
-            nc.vector.tensor_scalar_mul(out=other[:], in0=other[:], scalar1=neg_gain[:, c : c + 1, 1])
-            for syn, dst in enumerate((own, other)):
-                nc.vector.scalar_tensor_tensor(
-                    out=dst[:],
-                    in0=v_own,
-                    scalar=reversal[:, syn, c : c + 1],
-                    in1=dst[:],
-                    op0=ALU.subtract,
-                    op1=ALU.mult,
-                )
-            self_term[h, jb, e] = own
-            partner_term[h, jb, e] = other
-
-        for h in range(HALVES):
-            for jb in range(PAIR_BLOCKS):
-                for e in range(2):
-                    currents(h, jb, e)
-
-        def finish_rows(t):
+        def row_layout(t):
             h, lanes = t // TILES_PER_HALF, slice(P * (t % TILES_PER_HALF), P * (t % TILES_PER_HALF + 1))
-            neg_mean_parts = small.tile([P, 2], F32, name="neg_mean_parts")
-            x_banks = []
             for k in range(2):
                 bank = new_bank("x_bank")
-                for e in range(2):
-                    for jl in range(2):
-                        jb = 2 * k + jl
-                        block = slice(P * (2 * jl + e), P * (2 * jl + e + 1))
-                        parts = (self_term[h, jb, e], partner_term[h, jb, e], drive[h, jb, e])
-                        for i, part in enumerate(parts):
-                            nc.tensor.matmul(
-                                out=bank[:, block],
-                                lhsT=part[:, lanes],
-                                rhs=ident_f32[:],
-                                is_transpose=True,
-                                start=(i == 0),
-                                stop=(i == len(parts) - 1),
-                            )
+                for b in range(PACK):
+                    c = PACK * k + b
+                    parts = terms_of[h, c] + (drive[h, c],)
+                    for i, part in enumerate(parts):
+                        nc.tensor.matmul(
+                            out=bank[:, P * b : P * (b + 1)],
+                            lhsT=part[:, lanes],
+                            rhs=ident_f32[:],
+                            is_transpose=True,
+                            start=(i == 0),
+                            stop=(i == len(parts) - 1),
+                        )
+                x_banks[t, k] = bank
+
+        def row_mean(t):
+            neg_mean_parts = small.tile([P, 2], F32, name="neg_mean_parts")
+            for k in range(2):
                 unused = unused_pool.tile([P, BANK], BF16, name="unused")
                 nc.scalar.activation(
                     out=unused[:],
-                    in_=bank[:],
+                    in_=x_banks[t, k][:],
                     func=FUNC.Identity,
                     scale=-1.0 / CELLS,
                     accum_out=neg_mean_parts[:, k : k + 1],
                 )
-                x_banks.append(bank)
-            neg_mean = small.tile([P, 1], F32, name="neg_mean")
+            neg_mean[t] = small.tile([P, 1], F32, name="neg_mean")
             nc.scalar.activation(
-                out=neg_mean[:],
+                out=neg_mean[t][:],
                 in_=neg_mean_parts[:, 0:1],
                 func=FUNC.Identity,
                 bias=neg_mean_parts[:, 1:2],
             )
+
+        def row_rstd(t):
             square_parts = small.tile([P, 2], F32, name="square_parts")
             for k in range(2):
                 unused = unused_pool.tile([P, BANK], BF16, name="unused")
                 nc.scalar.activation(
                     out=unused[:],
-                    in_=x_banks[k][:],
+                    in_=x_banks[t, k][:],
                     func=FUNC.Square,
-                    bias=neg_mean[:, 0:1],
+                    bias=neg_mean[t][:, 0:1],
                     accum_out=square_parts[:, k : k + 1],
                 )
             part_eps = small.tile([P, 1], F32, name="part_eps")
@@ -464,29 +515,67 @@ def tile_memorylayercell_pa_kernel(
                 scale=1.0 / CELLS,
                 bias=part_eps[:, 0:1],
             )
-            rstd = small.tile([P, 1], F32, name="rstd")
-            nc.gpsimd.tensor_tensor(out=rstd[:], in0=var_eps[:], in1=neg_half[:], op=ALU.pow)
-            centred = row_pool.tile([P, CELLS], F32, name="centred")
+            rstd[t] = small.tile([P, 1], F32, name="rstd")
+            nc.gpsimd.tensor_tensor(out=rstd[t][:], in0=var_eps[:], in1=neg_half[:], op=ALU.pow)
+
+        def centre(t):
+            centred[t] = row_pool.tile([P, CELLS], F32, name="centred")
             for k in range(2):
                 cells = slice(BANK * k, BANK * (k + 1))
                 nc.vector.scalar_tensor_tensor(
-                    out=centred[:, cells].rearrange("p (m b) -> p m b", b=4),
-                    in0=x_banks[k][:].rearrange("p (b m) -> p m b", b=4),
-                    scalar=neg_mean[:, 0:1],
-                    in1=gamma_rows[:, cells].rearrange("p (m b) -> p m b", b=4),
+                    out=centred[t][:, cells].rearrange("p (m b) -> p m b", b=PACK),
+                    in0=x_banks[t, k][:].rearrange("p (b m) -> p m b", b=PACK),
+                    scalar=neg_mean[t][:, 0:1],
+                    in1=gamma_rows[:, cells].rearrange("p (m b) -> p m b", b=PACK),
                     op0=ALU.add,
                     op1=ALU.mult,
                 )
+
+        def store_rows(t):
             result = row_pool.tile([P, CELLS], F32, name="result")
             nc.vector.scalar_tensor_tensor(
                 out=result[:],
-                in0=centred[:],
-                scalar=rstd[:, 0:1],
+                in0=centred[t][:],
+                scalar=rstd[t][:, 0:1],
                 in1=beta_rows[:],
                 op0=ALU.mult,
                 op1=ALU.add,
             )
             nc.sync.dma_start(out=out_rows[:, t, :], in_=result[:])
 
+        for jb in range(PAIR_BLOCKS):
+            second_product(0, jb)
+        for g in (1, 2, 0):
+            quantise_cat(g, 1)
+        for c in range(N_COLS):
+            partner_gain(0, c)
+            product(0, c, 0)
+            product(0, c, 1)
+        for c in range(0, N_COLS, 2):
+            sigmoids(terms, 1, c)
+            sigmoids(terms, 1, c + 1)
+            self_gain(1, c)
+            self_gain(1, c + 1)
+        for g2 in range(PASSES_2):
+            for t in range(TILES_PER_HALF, ROW_TILES):
+                first_product(g2, t)
+                add_b1(g2, t)
+            quantise_h(g2, 1)
+        for jb in range(PAIR_BLOCKS):
+            second_product(1, jb)
+        row_layout(0)
+        row_mean(0)
         for t in range(ROW_TILES):
-            finish_rows(t)
+            if t < TILES_PER_HALF:
+                for c in (2 * t, 2 * t + 1):
+                    partner_gain(1, c)
+                    product(1, c, 0)
+                    product(1, c, 1)
+            if t + 1 < ROW_TILES:
+                row_layout(t + 1)
+                row_mean(t + 1)
+            row_rstd(t)
+            centre(t)
+            if t > 0:
+                store_rows(t - 1)
+        store_rows(ROW_TILES - 1)

@@ -188,7 +188,7 @@ def tile_memorylayercell_pa_kernel(
                     in_=bank[:].rearrange("p (q r) -> p q r", q=4)[:, :, 0 : 2 * arrays],
                 )
                 wide = consts.tile([P, arrays, N_COLS, 2], F32, name=name)
-                nc.gpsimd.tensor_copy(
+                nc.vector.tensor_copy(
                     out=wide[:].rearrange("p a (k q) s -> p (a k) q s", k=2),
                     in_=taken[:]
                     .rearrange("p q r -> p (q r)")
@@ -203,10 +203,9 @@ def tile_memorylayercell_pa_kernel(
             mean_pot = first_cells[:, 0, :, :]
             slope = first_cells[:, 1, :, :]
             shift = consts.tile([P, N_COLS, 2], F32)
-            nc.gpsimd.tensor_scalar(
-                out=shift[:], in0=mean_pot, scalar1=-1.0, scalar2=1.0, op0=ALU.mult, op1=ALU.mult
+            nc.vector.scalar_tensor_tensor(
+                out=shift[:], in0=slope, scalar=-1.0, in1=mean_pot, op0=ALU.mult, op1=ALU.mult
             )
-            nc.gpsimd.tensor_tensor(out=shift[:], in0=shift[:], in1=slope, op=ALU.mult)
 
             w1_codes = keep.tile([P, PASSES_1, CELLS], U32, align_bytes=64)
             w1_scales = keep.tile([P, PASSES_1, CELLS], U8, align_bytes=64)
@@ -367,12 +366,12 @@ def tile_memorylayercell_pa_kernel(
                 .rearrange("p (u r e) -> p r u e", u=3, e=2)
             )
             vecs = consts.tile([P, 4, N_COLS], F32)
-            nc.gpsimd.tensor_copy(
+            nc.vector.tensor_copy(
                 out=vecs[:].rearrange("p v (k u e) -> p (v k) u e", k=2, u=2),
                 in_=vec_halves[:, 0:8, 0:2, :],
             )
             b2_cols = consts.tile([P, PAIR_BLOCKS], F32)
-            nc.gpsimd.tensor_copy(
+            nc.vector.tensor_copy(
                 out=b2_cols[:].rearrange("p (k u) -> p k u", k=2), in_=vec_halves[:, 8:10, 2, :]
             )
             reversal = vecs[:, 0:2, :]
@@ -380,32 +379,27 @@ def tile_memorylayercell_pa_kernel(
             inv_cap = consts.tile([P, N_COLS], F32)
             nc.vector.reciprocal(out=inv_cap[:], in_=vecs[:, 2, :])
             neg_inv = consts.tile([P, N_COLS], F32)
-            nc.gpsimd.tensor_scalar(
-                out=neg_inv[:], in0=inv_cap[:], scalar1=-1.0, scalar2=1.0, op0=ALU.mult, op1=ALU.mult
-            )
+            nc.vector.tensor_scalar_mul(out=neg_inv[:], in0=inv_cap[:], scalar1=-1.0)
             neg_gain = consts.tile([P, N_COLS, 2], F32)
-            nc.gpsimd.tensor_tensor(
+            nc.vector.tensor_tensor(
                 out=neg_gain[:],
                 in0=max_cond,
                 in1=neg_inv[:].unsqueeze(2).to_broadcast([P, N_COLS, 2]),
                 op=ALU.mult,
             )
             drive_gain = consts.tile([P, N_COLS], F32)
-            nc.gpsimd.tensor_copy(out=drive_gain[:, 0:N_COLS:2], in_=inv_cap[:, 0:N_COLS:2])
-            nc.gpsimd.tensor_copy(out=drive_gain[:, 1:N_COLS:2], in_=neg_inv[:, 1:N_COLS:2])
+            nc.vector.tensor_copy(out=drive_gain[:, 0:N_COLS:2], in_=inv_cap[:, 0:N_COLS:2])
+            nc.vector.tensor_copy(out=drive_gain[:, 1:N_COLS:2], in_=neg_inv[:, 1:N_COLS:2])
             drive_bias = consts.tile([P, N_COLS], F32)
-            nc.gpsimd.tensor_tensor(
+            nc.vector.tensor_tensor(
                 out=drive_bias[:].rearrange("p (j e) -> p j e", e=2),
                 in0=drive_gain[:].rearrange("p (j e) -> p j e", e=2),
                 in1=b2_cols[:].unsqueeze(2).to_broadcast([P, PAIR_BLOCKS, 2]),
                 op=ALU.mult,
             )
-            nc.gpsimd.tensor_tensor(
+            nc.vector.tensor_tensor(
                 out=drive_bias[:], in0=drive_bias[:], in1=vecs[:, 0, :], op=ALU.add
             )
-            neg_half = consts.tile([P, 1], F32)
-            nc.gpsimd.memset(neg_half[:], -0.5)
-
             for g in (1, 2, 0):
                 for t0 in range(TILES_PER_HALF, ROW_TILES, 2):
                     transpose_cat(g, t0)
@@ -507,16 +501,14 @@ def tile_memorylayercell_pa_kernel(
             nc.scalar.activation(
                 out=part_eps[:], in_=square_parts[:, 1:2], func=FUNC.Identity, scale=1.0 / CELLS, bias=EPS
             )
-            var_eps = small.tile([P, 1], F32, name="var_eps")
+            rstd[t] = small.tile([P, 1], F32, name="rstd")
             nc.scalar.activation(
-                out=var_eps[:],
+                out=rstd[t][:],
                 in_=square_parts[:, 0:1],
-                func=FUNC.Identity,
+                func=FUNC.Abs_reciprocal_sqrt,
                 scale=1.0 / CELLS,
                 bias=part_eps[:, 0:1],
             )
-            rstd[t] = small.tile([P, 1], F32, name="rstd")
-            nc.gpsimd.tensor_tensor(out=rstd[t][:], in0=var_eps[:], in1=neg_half[:], op=ALU.pow)
 
         def centre(t):
             centred[t] = row_pool.tile([P, CELLS], F32, name="centred")

@@ -453,6 +453,13 @@ def tile_memorylayercell_pa_kernel(
             h, lanes = t // TILES_PER_HALF, slice(P * (t % TILES_PER_HALF), P * (t % TILES_PER_HALF + 1))
             for k in range(2):
                 bank = new_bank("x_bank")
+                nc.tensor.matmul(
+                    out=bank[:, 0 : 2 * P],
+                    lhsT=ident_f32[:],
+                    rhs=drive[h, PACK * k][:, 0 : 2 * P],
+                    start=True,
+                    stop=True,
+                )
                 for b in range(PACK):
                     c = PACK * k + b
                     parts = terms_of[h, c] + (drive[h, c],)

@@ -454,9 +454,9 @@ def tile_memorylayercell_pa_kernel(
             for k in range(2):
                 bank = new_bank("x_bank")
                 nc.tensor.matmul(
-                    out=bank[:, 0 : 2 * P],
-                    lhsT=ident_f32[:],
-                    rhs=drive[h, PACK * k][:, 0 : 2 * P],
+                    out=bank[:],
+                    lhsT=first_rows[:, 0:P],
+                    rhs=first_rows[:, 0:BANK],
                     start=True,
                     stop=True,
                 )

@@ -101,26 +101,21 @@ def tile_memorylayercell_pa_kernel(
                 tiles = slice(t0, t0 + n)
                 nc.sync.dma_start(out=inputs_nat[:, tiles, :], in_=inputs_rows[:, tiles, :])
 
-            def load_w1(g, first, width):
-                cols = slice(first, first + width)
-                raw = w_raw_pool.tile([P, PACK, width], BF16, name="w1_raw_%d_%d" % (g, first))
+            def load_w1(g):
+                raw = w_raw_pool.tile([P, PACK, CELLS], BF16, name="w1_raw_%d" % g)
                 nc.sync.dma_start(
                     out=raw[:],
-                    in_=W1[K_PASS * g : K_PASS * (g + 1), cols].rearrange("(q t) s -> q t s", t=PACK),
+                    in_=W1[K_PASS * g : K_PASS * (g + 1), :].rearrange("(q t) s -> q t s", t=PACK),
                 )
-                for g2 in range(first // K_PASS, (first + width) // K_PASS):
-                    w1_raw[g, g2] = raw[:, :, K_PASS * g2 - first : K_PASS * (g2 + 1) - first]
+                w1_raw[g] = raw
 
             w1_raw = {}
             w2_raw = w_raw_pool.tile([P, PASSES_2, PACK, PAIRS], BF16, name="w2_raw")
-            load_w1(0, 0, K_PASS)
-            load_states(0, 2)
-            load_w1(0, K_PASS, K_PASS)
-            load_states(2, 2)
-            load_w1(1, 0, K_PASS)
+            load_w1(0)
+            load_states(0, TILES_PER_HALF)
+            load_w1(1)
             load_inputs(0, TILES_PER_HALF)
-            load_w1(1, K_PASS, K_PASS)
-            load_w1(2, 0, CELLS)
+            load_w1(2)
             nc.sync.dma_start(
                 out=later_rows[0:2, :], in_=max_conductance.rearrange("(k c) s -> k (c s)", k=2)
             )
@@ -216,7 +211,7 @@ def tile_memorylayercell_pa_kernel(
                 cols = slice(K_PASS * g2, K_PASS * (g2 + 1))
                 nc.vector.tensor_copy(
                     out=w1_grouped[g][:, cols, :].rearrange("p (i m) t -> p m t i", i=PACK),
-                    in_=w1_raw[g, g2].rearrange("p t (m i) -> p m t i", i=PACK),
+                    in_=w1_raw[g][:, :, cols].rearrange("p t (m i) -> p m t i", i=PACK),
                 )
 
             def quantise_w1(g, g2):

@@ -53,53 +53,238 @@ def tile_memorylayercell_pa_kernel(
 ):
     nc = tc.nc
     with ExitStack() as ctx:
+        ctx.enter_context(tc.manual_schedule())
         consts = ctx.enter_context(tc.tile_pool(name="consts", bufs=1))
-        gamma_rows = consts.tile([P, CELLS], BF16)
-        beta_rows = consts.tile([P, CELLS], BF16)
         keep = ctx.enter_context(tc.tile_pool(name="keep", bufs=1))
         terms = ctx.enter_context(tc.tile_pool(name="terms", bufs=1))
-        small = ctx.enter_context(tc.tile_pool(name="small", bufs=4))
+        small = ctx.enter_context(tc.tile_pool(name="small", bufs=6))
         psum = ctx.enter_context(tc.psum_pool(name="psum", bufs=8))
 
         def new_bank(label):
             return psum.tile([P, BANK], F32, name=label, tag="bank")
 
-
         first_rows = consts.tile([P, 8 * P], BF16)
-        later_rows = consts.tile([P, 8 * P], BF16)
-        nc.gpsimd.memset(first_rows[:].bitcast(F32), 0.0)
         for a, mat in enumerate((mean_conductance_potential, std_conductance)):
-            nc.scalar.dma_start(
-                out=first_rows[2 * a : 2 * a + 2, :],
-                in_=mat.rearrange("(k c) s -> k (c s)", k=2),
-            )
-
-        table_probe = consts.tile([P, 1], F32)
-        nc.vector.memset(table_probe[:], 0.0)
-        nc.scalar.activation(out=table_probe[:], in_=table_probe[:], func=FUNC.Sigmoid)
+            for k in range(2):
+                first = 64 * a + 32 * k
+                nc.scalar.dma_start(
+                    out=first_rows[first : first + 32, :],
+                    in_=mat[4 * P * k : 4 * P * (k + 1), :]
+                    .rearrange("c s -> (c s)")
+                    .partition_broadcast(32),
+                )
+        later_rows = consts.tile([P, 8 * P], BF16)
         ident_f32 = consts.tile([P, P], F32)
         make_identity(nc, ident_f32[:])
         nc.gpsimd.memset(later_rows[:].bitcast(F32), 0.0)
+        sign = consts.tile([P, PAIR_BLOCKS, 2], F32)
+        nc.gpsimd.memset(sign[:, :, 0], 1.0)
+        nc.gpsimd.memset(sign[:, :, 1], -1.0)
+        table_probe = consts.tile([P, 1], F32)
+        nc.vector.memset(table_probe[:], 0.0)
+        nc.scalar.activation(out=table_probe[:], in_=table_probe[:], func=FUNC.Sigmoid)
+
+        mats = consts.tile([P, 2, N_COLS, 2], F32)
+        mean_pot = mats[:, 0, :, :]
+        slope = mats[:, 1, :, :]
+        shift = consts.tile([P, N_COLS, 2], F32)
+        max_cond = consts.tile([P, N_COLS, 2], F32)
+        vecs = consts.tile([P, 4, N_COLS], F32)
+        reversal = vecs[:, 0:2, :]
+        b1_cols = vecs[:, 3, :].rearrange("p (g t) -> p g t", g=PASSES_2)
+        inv_cap = consts.tile([P, N_COLS], F32)
+        neg_gain = consts.tile([P, N_COLS, 2], F32)
+        drive_gain = consts.tile([P, N_COLS], F32)
+        drive_bias = consts.tile([P, N_COLS], F32)
+        const_banks = {}
+
+        def transpose_cells(rows, label):
+            const_banks[label] = new_bank(label)
+            for q in range(4):
+                nc.tensor.transpose(
+                    const_banks[label][:, P * q : P * (q + 1)], rows[:, q : 4 * P : 4], ident_f32[:]
+                )
+
+        def bank_halves(label, blocks):
+            return const_banks[label][:].bitcast(BF16)[:, 0 : 2 * P * blocks].rearrange(
+                "p (q r s) -> p r q s", q=blocks, s=2
+            )
+
+        def widen_first():
+            nc.vector.tensor_copy(
+                out=mats[:].rearrange("p a (k q) s -> p (a k) q s", k=2),
+                in_=bank_halves("first_bank", 4)[:, 0 : 4 * 32 : 32, :, :],
+            )
+
+        def make_shift():
+            nc.vector.scalar_tensor_tensor(
+                out=shift[:], in0=slope, scalar=-1.0, in1=mean_pot, op0=ALU.mult, op1=ALU.mult
+            )
+
+        def widen_max_cond():
+            nc.vector.tensor_copy(
+                out=max_cond[:].rearrange("p (k q) s -> p k q s", k=2),
+                in_=bank_halves("gain_bank", 4)[:, 0:2, :, :],
+            )
+
+        def widen_vecs():
+            nc.vector.tensor_copy(
+                out=vecs[:].rearrange("p v (k u e) -> p (v k) u e", k=2, u=2),
+                in_=bank_halves("vec_bank", 3)[:, 2:10, 0:2, :],
+            )
+
+        def make_inv_cap():
+            nc.vector.reciprocal(out=inv_cap[:], in_=vecs[:, 2, :])
+
+        def make_neg_gain():
+            nc.vector.scalar_tensor_tensor(
+                out=neg_gain[:],
+                in0=max_cond[:],
+                scalar=-1.0,
+                in1=inv_cap[:].unsqueeze(2).to_broadcast([P, N_COLS, 2]),
+                op0=ALU.mult,
+                op1=ALU.mult,
+            )
+
+        def make_drive_gain():
+            nc.vector.tensor_mul(
+                out=drive_gain[:], in0=inv_cap[:], in1=sign[:].rearrange("p j e -> p (j e)")
+            )
+
+        def start_drive_bias():
+            b2_pairs = bank_halves("vec_bank", 3)[:, 10:12, 2, :]
+            nc.vector.tensor_mul(
+                out=drive_bias[:].rearrange("p (k u e) -> p k u e", k=2, u=2),
+                in0=drive_gain[:].rearrange("p (k u e) -> p k u e", k=2, u=2),
+                in1=b2_pairs.unsqueeze(3).to_broadcast([P, 2, 2, 2]),
+            )
+
+        def finish_drive_bias():
+            nc.vector.tensor_add(out=drive_bias[:], in0=drive_bias[:], in1=vecs[:, 0, :])
+
+        cat_grouped = keep.tile([P, PASSES_1, ROWS, PACK], BF16, align_bytes=64)
+        cat_codes = keep.tile([P, PASSES_1, ROWS], U32, align_bytes=64)
+        cat_scales = keep.tile([P, PASSES_1, ROWS], U8, align_bytes=64)
+        cat_words = cat_grouped[:].bitcast(F32)
+        w1_codes = keep.tile([P, PASSES_1, CELLS], U32, align_bytes=64)
+        w1_scales = keep.tile([P, PASSES_1, CELLS], U8, align_bytes=64)
+        w2_codes = keep.tile([P, PASSES_2, PAIRS], U32, align_bytes=64)
+        w2_scales = keep.tile([P, PASSES_2, PAIRS], U8, align_bytes=64)
+        h_grouped = keep.tile([P, PASSES_2, ROWS, PACK], BF16, align_bytes=64)
+        h_codes = keep.tile([P, PASSES_2, ROWS], U32, align_bytes=64)
+        h_scales = keep.tile([P, PASSES_2, ROWS], U8, align_bytes=64)
+        gamma_rows = consts.tile([P, CELLS], BF16)
+        beta_rows = consts.tile([P, CELLS], BF16)
+
+        h_banks = {}
+
+        def quantise_cat(g, h):
+            rows = slice(HALF * h, HALF * (h + 1))
+            nc.vector.quantize_mx(
+                out=cat_codes[:, g, rows].bitcast(FP8X4),
+                scales=cat_scales[:, g, rows],
+                in_=cat_grouped[:, g, rows, :].rearrange("p r t -> p (r t)"),
+            )
+
+        def first_product(g2, t):
+            rows = slice(P * t, P * (t + 1))
+            bank = new_bank("h_bank")
+            for t4 in range(PACK):
+                cols = slice(K_PASS * g2 + P * t4, K_PASS * g2 + P * (t4 + 1))
+                for g in range(PASSES_1):
+                    nc.tensor.matmul_mx(
+                        out=bank[:, P * t4 : P * (t4 + 1)],
+                        lhsT=w1_codes[:, g, cols].bitcast(FP8X4),
+                        lhsT_scale=w1_scales[:, g, cols],
+                        rhs=cat_codes[:, g, rows].bitcast(FP8X4),
+                        rhs_scale=cat_scales[:, g, rows],
+                        start=(g == 0),
+                        stop=(g == PASSES_1 - 1),
+                    )
+            h_banks[g2, t] = bank
+
+        def add_b1(g2, t):
+            nc.vector.tensor_tensor(
+                out=h_grouped[:, g2, P * t : P * (t + 1), :],
+                in0=h_banks[g2, t][:].rearrange("p (t r) -> p r t", t=PACK),
+                in1=b1_cols[:, g2, :].unsqueeze(1).to_broadcast([P, P, PACK]),
+                op=ALU.add,
+            )
+
+        def quantise_h(g2, h):
+            rows = slice(HALF * h, HALF * (h + 1))
+            nc.vector.quantize_mx(
+                out=h_codes[:, g2, rows].bitcast(FP8X4),
+                scales=h_scales[:, g2, rows],
+                in_=h_grouped[:, g2, rows, :].rearrange("p r t -> p (r t)"),
+            )
+
+        terms_of = {}
+
+        def sigmoids(h, c):
+            rows = slice(HALF * h, HALF * (h + 1))
+            g, b = 1 + c // PACK, c % PACK
+            own = terms.tile([P, HALF], F32, name="self_%d_%d" % (h, c))
+            other = terms.tile([P, HALF], F32, name="partner_%d_%d" % (h, c))
+            partner = b + 1 - 2 * (b % 2)
+            for syn, dst, value in ((1, other, partner), (0, own, b)):
+                nc.scalar.activation(
+                    out=dst[:],
+                    in_=cat_grouped[:, g, rows, value],
+                    func=FUNC.Sigmoid,
+                    scale=slope[:, c : c + 1, syn],
+                    bias=shift[:, c : c + 1, syn],
+                )
+            terms_of[h, c] = (own, other)
+
+        def self_gain(h, c):
+            own = terms_of[h, c][0]
+            nc.scalar.activation(
+                out=own[:], in_=own[:], func=FUNC.Identity, scale=neg_gain[:, c : c + 1, 0], bias=1.0
+            )
+
+        def partner_gain(h, c):
+            other = terms_of[h, c][1]
+            nc.vector.tensor_scalar_mul(out=other[:], in0=other[:], scalar1=neg_gain[:, c : c + 1, 1])
+
+        def product(h, c, syn):
+            dst = terms_of[h, c][syn]
+            rows = slice(HALF * h, HALF * (h + 1))
+            nc.vector.scalar_tensor_tensor(
+                out=dst[:],
+                in0=cat_grouped[:, 1 + c // PACK, rows, c % PACK],
+                scalar=reversal[:, syn, c : c + 1],
+                in1=dst[:],
+                op0=ALU.subtract,
+                op1=ALU.mult,
+            )
+
+        def products(h, c):
+            if c + 1 < N_COLS:
+                partner_gain(h, c + 1)
+            product(h, c, 1)
+            product(h, c, 0)
+
+        units = {
+            h: [(g2, TILES_PER_HALF * h + i) for g2 in range(PASSES_2) for i in range(TILES_PER_HALF)]
+            for h in range(HALVES)
+        }
 
         with (
             tc.tile_pool(name="natural", bufs=1) as natural,
             tc.tile_pool(name="w_raw", bufs=1) as w_raw_pool,
             tc.tile_pool(name="w_grouped", bufs=2) as w_grouped_pool,
         ):
-
             states_rows = states.rearrange("(p t) s -> p t s", t=ROW_TILES)
             inputs_rows = inputs.rearrange("(p t) s -> p t s", t=ROW_TILES)
-            out_rows = out.rearrange("(p t) s -> p t s", t=ROW_TILES)
             states_nat = natural.tile([P, ROW_TILES, CELLS], BF16)
             inputs_nat = natural.tile([P, ROW_TILES, D_IN], BF16)
+            inputs_words = inputs_nat[:].bitcast(F32)
+            states_words = states_nat[:].bitcast(F32)
 
-            def load_states(t0, n):
-                tiles = slice(t0, t0 + n)
-                nc.sync.dma_start(out=states_nat[:, tiles, :], in_=states_rows[:, tiles, :])
-
-            def load_inputs(t0, n):
-                tiles = slice(t0, t0 + n)
-                nc.sync.dma_start(out=inputs_nat[:, tiles, :], in_=inputs_rows[:, tiles, :])
+            def load_rows(nat, rows, h):
+                tiles = slice(TILES_PER_HALF * h, TILES_PER_HALF * (h + 1))
+                nc.sync.dma_start(out=nat[:, tiles, :], in_=rows[:, tiles, :])
 
             def load_w1(g):
                 raw = w_raw_pool.tile([P, PACK, CELLS], BF16, name="w1_raw_%d" % g)
@@ -110,11 +295,10 @@ def tile_memorylayercell_pa_kernel(
                 w1_raw[g] = raw
 
             w1_raw = {}
-            w2_raw = w_raw_pool.tile([P, PASSES_2, PACK, PAIRS], BF16, name="w2_raw")
             load_w1(0)
-            load_states(0, TILES_PER_HALF)
+            load_rows(states_nat, states_rows, 0)
             load_w1(1)
-            load_inputs(0, TILES_PER_HALF)
+            load_rows(inputs_nat, inputs_rows, 0)
             load_w1(2)
             nc.sync.dma_start(
                 out=later_rows[0:2, :], in_=max_conductance.rearrange("(k c) s -> k (c s)", k=2)
@@ -127,20 +311,16 @@ def tile_memorylayercell_pa_kernel(
             nc.sync.dma_start(
                 out=later_rows[10:12, 0 : 2 * P], in_=b2.rearrange("(k c) -> k c", k=2)
             )
-            load_states(TILES_PER_HALF, TILES_PER_HALF)
+            load_rows(states_nat, states_rows, 1)
+            w2_raw = w_raw_pool.tile([P, PASSES_2, PACK, PAIRS], BF16, name="w2_raw")
             nc.sync.dma_start(
                 out=w2_raw[:], in_=W2.rearrange("(g p t) n -> p g t n", g=PASSES_2, t=PACK)
             )
-            load_inputs(TILES_PER_HALF, TILES_PER_HALF)
+            load_rows(inputs_nat, inputs_rows, 1)
             nc.sync.dma_start(out=gamma_rows[:], in_=gamma.partition_broadcast(P))
             nc.sync.dma_start(out=beta_rows[:], in_=beta.partition_broadcast(P))
 
-            cat_grouped = keep.tile([P, PASSES_1, ROWS, PACK], BF16, align_bytes=64)
-            cat_codes = keep.tile([P, PASSES_1, ROWS], U32, align_bytes=64)
-            cat_scales = keep.tile([P, PASSES_1, ROWS], U8, align_bytes=64)
-            cat_words = cat_grouped[:].bitcast(F32)
-            inputs_words = inputs_nat[:].bitcast(F32)
-            states_words = states_nat[:].bitcast(F32)
+            cat_banks = {}
 
             def transpose_cat(g, t0):
                 bank = new_bank("cat_bank")
@@ -154,60 +334,21 @@ def tile_memorylayercell_pa_kernel(
                         nc.tensor.transpose(
                             bank[:, P * (2 * u + i) : P * (2 * u + i + 1)], words, ident_f32[:]
                         )
+                cat_banks[g, t0] = bank
+
+            def copy_cat(g, t0):
                 nc.scalar.copy(
                     out=cat_words[:, g, P * t0 : P * (t0 + 2), :],
-                    in_=bank[:].rearrange("p (u r) -> p r u", u=2),
+                    in_=cat_banks[g, t0][:].rearrange("p (u r) -> p r u", u=2),
                 )
 
-            def quantise_cat(g, h):
-                rows = slice(HALF * h, HALF * (h + 1))
-                nc.vector.quantize_mx(
-                    out=cat_codes[:, g, rows].bitcast(FP8X4),
-                    scales=cat_scales[:, g, rows],
-                    in_=cat_grouped[:, g, rows, :].rearrange("p r t -> p (r t)"),
-                )
-
-            for g in (1, 2):
-                transpose_cat(g, 0)
-
-            def transpose_cells(bank, rows):
-                for q in range(4):
-                    nc.tensor.transpose(
-                        bank[:, P * q : P * (q + 1)], rows[:, q : 4 * P : 4], ident_f32[:]
-                    )
-
-            def widen_cells(name, bank, arrays):
-                taken = consts.tile([P, 4, 2 * arrays], F32, name=name + "_words")
-                nc.vector.tensor_copy(
-                    out=taken[:],
-                    in_=bank[:].rearrange("p (q r) -> p q r", q=4)[:, :, 0 : 2 * arrays],
-                )
-                wide = consts.tile([P, arrays, N_COLS, 2], F32, name=name)
-                nc.vector.tensor_copy(
-                    out=wide[:].rearrange("p a (k q) s -> p (a k) q s", k=2),
-                    in_=taken[:]
-                    .rearrange("p q r -> p (q r)")
-                    .bitcast(BF16)
-                    .rearrange("p (q r s) -> p r q s", q=4, s=2),
-                )
-                return wide
-
-            first_bank = new_bank("first_bank")
-            transpose_cells(first_bank, first_rows[:].bitcast(F32))
-            first_cells = widen_cells("first_cells", first_bank, 2)
-            mean_pot = first_cells[:, 0, :, :]
-            slope = first_cells[:, 1, :, :]
-            shift = consts.tile([P, N_COLS, 2], F32)
-            nc.vector.scalar_tensor_tensor(
-                out=shift[:], in0=slope, scalar=-1.0, in1=mean_pot, op0=ALU.mult, op1=ALU.mult
-            )
-
-            w1_codes = keep.tile([P, PASSES_1, CELLS], U32, align_bytes=64)
-            w1_scales = keep.tile([P, PASSES_1, CELLS], U8, align_bytes=64)
-            w2_codes = keep.tile([P, PASSES_2, PAIRS], U32, align_bytes=64)
-            w2_scales = keep.tile([P, PASSES_2, PAIRS], U8, align_bytes=64)
+            w1_grouped = {}
 
             def regroup_w1(g, g2):
+                if g2 == 0:
+                    w1_grouped[g] = w_grouped_pool.tile(
+                        [P, CELLS, PACK], BF16, name="w1_grouped", tag="w_grouped", align_bytes=64
+                    )
                 cols = slice(K_PASS * g2, K_PASS * (g2 + 1))
                 nc.vector.tensor_copy(
                     out=w1_grouped[g][:, cols, :].rearrange("p (i m) t -> p m t i", i=PACK),
@@ -222,199 +363,109 @@ def tile_memorylayercell_pa_kernel(
                     in_=w1_grouped[g][:, cols, :].rearrange("p c t -> p (c t)"),
                 )
 
-            w1_grouped = []
-            for g in range(PASSES_1):
-                grouped = w_grouped_pool.tile(
-                    [P, CELLS, PACK], BF16, name="w1_grouped", tag="w_grouped", align_bytes=64
+            w2_grouped = []
+
+            def regroup_w2(g):
+                if g == 0:
+                    w2_grouped.append(
+                        w_grouped_pool.tile(
+                            [P, PASSES_2, PAIRS, PACK], BF16, name="w2_grouped", tag="w_grouped", align_bytes=64
+                        )
+                    )
+                nc.vector.tensor_copy(
+                    out=w2_grouped[0][:, g, :, :].rearrange("p (k u m) t -> p k m t u", k=2, u=2),
+                    in_=w2_raw[:, g, :, :].rearrange("p t (k m u) -> p k m t u", k=2, u=2),
                 )
-                w1_grouped.append(grouped)
 
             def quantise_w2():
-                w2_grouped = w_grouped_pool.tile(
-                    [P, PASSES_2, PAIRS, PACK], BF16, name="w2_grouped", tag="w_grouped", align_bytes=64
-                )
-                for g in range(PASSES_2):
-                    nc.vector.tensor_copy(
-                        out=w2_grouped[:, g, :, :].rearrange("p (k u m) t -> p k m t u", k=2, u=2),
-                        in_=w2_raw[:, g, :, :].rearrange("p t (k m u) -> p k m t u", k=2, u=2),
-                    )
                 nc.vector.quantize_mx(
                     out=w2_codes[:].rearrange("p g c -> p (g c)").bitcast(FP8X4),
                     scales=w2_scales[:].rearrange("p g c -> p (g c)"),
-                    in_=w2_grouped[:].rearrange("p g c t -> p (g c t)"),
+                    in_=w2_grouped[0][:].rearrange("p g c t -> p (g c t)"),
                 )
 
-            h_grouped = keep.tile([P, PASSES_2, ROWS, PACK], BF16, align_bytes=64)
-            h_codes = keep.tile([P, PASSES_2, ROWS], U32, align_bytes=64)
-            h_scales = keep.tile([P, PASSES_2, ROWS], U8, align_bytes=64)
-
-            h_banks = {}
-
-            def first_product(g2, t):
-                rows = slice(P * t, P * (t + 1))
-                bank = new_bank("h_bank")
-                for t4 in range(PACK):
-                    cols = slice(K_PASS * g2 + P * t4, K_PASS * g2 + P * (t4 + 1))
-                    for g in range(PASSES_1):
-                        nc.tensor.matmul_mx(
-                            out=bank[:, P * t4 : P * (t4 + 1)],
-                            lhsT=w1_codes[:, g, cols].bitcast(FP8X4),
-                            lhsT_scale=w1_scales[:, g, cols],
-                            rhs=cat_codes[:, g, rows].bitcast(FP8X4),
-                            rhs_scale=cat_scales[:, g, rows],
-                            start=(g == 0),
-                            stop=(g == PASSES_1 - 1),
-                        )
-                h_banks[g2, t] = bank
-
-            def add_b1(g2, t):
-                rows = slice(P * t, P * (t + 1))
-                bank = h_banks[g2, t]
-                nc.vector.tensor_tensor(
-                    out=h_grouped[:, g2, rows, :],
-                    in0=bank[:].rearrange("p (t r) -> p r t", t=PACK),
-                    in1=b1_cols[:, g2, :].unsqueeze(1).to_broadcast([P, P, PACK]),
-                    op=ALU.add,
-                )
-
-            def quantise_h(g2, h):
-                rows = slice(HALF * h, HALF * (h + 1))
-                nc.vector.quantize_mx(
-                    out=h_codes[:, g2, rows].bitcast(FP8X4),
-                    scales=h_scales[:, g2, rows],
-                    in_=h_grouped[:, g2, rows, :].rearrange("p r t -> p (r t)"),
-                )
-
-            terms_of = {}
-
-            def sigmoids(pool, h, c):
-                rows = slice(HALF * h, HALF * (h + 1))
-                g, b = 1 + c // PACK, c % PACK
-                own = pool.tile([P, HALF], F32, name="self_%d_%d" % (h, c))
-                other = pool.tile([P, HALF], F32, name="partner_%d_%d" % (h, c))
-                partner = b + 1 - 2 * (b % 2)
-                for syn, dst, value in ((1, other, partner), (0, own, b)):
-                    nc.scalar.activation(
-                        out=dst[:],
-                        in_=cat_grouped[:, g, rows, value],
-                        func=FUNC.Sigmoid,
-                        scale=slope[:, c : c + 1, syn],
-                        bias=shift[:, c : c + 1, syn],
-                    )
-                terms_of[h, c] = (own, other)
-
-            def self_gain(h, c):
-                own = terms_of[h, c][0]
-                nc.scalar.activation(
-                    out=own[:], in_=own[:], func=FUNC.Identity, scale=neg_gain[:, c : c + 1, 0], bias=1.0
-                )
-
-            def partner_gain(h, c):
-                other = terms_of[h, c][1]
-                nc.vector.tensor_scalar_mul(
-                    out=other[:], in0=other[:], scalar1=neg_gain[:, c : c + 1, 1]
-                )
-
-            def product(h, c, syn):
-                dst = terms_of[h, c][syn]
-                rows = slice(HALF * h, HALF * (h + 1))
-                nc.vector.scalar_tensor_tensor(
-                    out=dst[:],
-                    in0=cat_grouped[:, 1 + c // PACK, rows, c % PACK],
-                    scalar=reversal[:, syn, c : c + 1],
-                    in1=dst[:],
-                    op0=ALU.subtract,
-                    op1=ALU.mult,
-                )
-
-            for g in (1, 2):
-                transpose_cat(g, 2)
+            for t0 in (0, 2):
+                for g in (1, 2):
+                    transpose_cat(g, t0)
+                    copy_cat(g, t0)
+            for g2 in range(PASSES_2):
+                regroup_w1(0, g2)
+            for g2 in range(PASSES_2):
+                quantise_w1(0, g2)
+            transpose_cells(first_rows[:].bitcast(F32), "first_bank")
             for t0 in (0, 2):
                 transpose_cat(0, t0)
-            for g in range(PASSES_1):
-                for g2 in range(PASSES_2):
-                    regroup_w1(g, g2)
-                for g2 in range(PASSES_2):
-                    quantise_w1(g, g2)
-                if g == 0:
-                    for g_cat in (1, 2, 0):
-                        quantise_cat(g_cat, 0)
+                copy_cat(0, t0)
+            regroup_w1(1, 0)
+            regroup_w1(1, 1)
+            widen_first()
+            quantise_w1(1, 0)
+            make_shift()
+            quantise_w1(1, 1)
+            quantise_cat(1, 0)
+            quantise_cat(2, 0)
+            for c in range(5):
+                sigmoids(0, c)
+
             later_words = later_rows[:].bitcast(F32)
-            gain_bank = new_bank("gain_bank")
-            transpose_cells(gain_bank, later_words)
-            vec_bank = new_bank("vec_bank")
+            transpose_cells(later_words, "gain_bank")
+            const_banks["vec_bank"] = new_bank("vec_bank")
             for u in range(2):
                 nc.tensor.transpose(
-                    vec_bank[:, P * u : P * (u + 1)], later_words[:, u : 2 * P : 2], ident_f32[:]
+                    const_banks["vec_bank"][:, P * u : P * (u + 1)], later_words[:, u : 2 * P : 2], ident_f32[:]
                 )
-            nc.tensor.transpose(vec_bank[:, 2 * P : 3 * P], later_words[:, 0:P], ident_f32[:])
-            max_cond = widen_cells("max_cond", gain_bank, 1)[:, 0, :, :]
-            vec_small = consts.tile([P, 3, 10], F32)
-            nc.vector.tensor_copy(
-                out=vec_small[:],
-                in_=vec_bank[:, 0 : 3 * P].rearrange("p (u r) -> p u r", u=3)[:, :, 2:12],
+            nc.tensor.transpose(
+                const_banks["vec_bank"][:, 2 * P : 3 * P], later_words[:, 0:P], ident_f32[:]
             )
-            vec_halves = (
-                vec_small[:]
-                .rearrange("p u r -> p (u r)")
-                .bitcast(BF16)
-                .rearrange("p (u r e) -> p r u e", u=3, e=2)
-            )
-            vecs = consts.tile([P, 4, N_COLS], F32)
-            nc.vector.tensor_copy(
-                out=vecs[:].rearrange("p v (k u e) -> p (v k) u e", k=2, u=2),
-                in_=vec_halves[:, 0:8, 0:2, :],
-            )
-            b2_cols = consts.tile([P, PAIR_BLOCKS], F32)
-            nc.vector.tensor_copy(
-                out=b2_cols[:].rearrange("p (k u) -> p k u", k=2), in_=vec_halves[:, 8:10, 2, :]
-            )
-            reversal = vecs[:, 0:2, :]
-            b1_cols = vecs[:, 3, :].rearrange("p (g t) -> p g t", g=PASSES_2)
-            inv_cap = consts.tile([P, N_COLS], F32)
-            nc.vector.reciprocal(out=inv_cap[:], in_=vecs[:, 2, :])
-            neg_inv = consts.tile([P, N_COLS], F32)
-            nc.vector.tensor_scalar_mul(out=neg_inv[:], in0=inv_cap[:], scalar1=-1.0)
-            neg_gain = consts.tile([P, N_COLS, 2], F32)
-            nc.vector.tensor_tensor(
-                out=neg_gain[:],
-                in0=max_cond,
-                in1=neg_inv[:].unsqueeze(2).to_broadcast([P, N_COLS, 2]),
-                op=ALU.mult,
-            )
-            drive_gain = consts.tile([P, N_COLS], F32)
-            nc.vector.tensor_copy(out=drive_gain[:, 0:N_COLS:2], in_=inv_cap[:, 0:N_COLS:2])
-            nc.vector.tensor_copy(out=drive_gain[:, 1:N_COLS:2], in_=neg_inv[:, 1:N_COLS:2])
-            drive_bias = consts.tile([P, N_COLS], F32)
-            nc.vector.tensor_tensor(
-                out=drive_bias[:].rearrange("p (j e) -> p j e", e=2),
-                in0=drive_gain[:].rearrange("p (j e) -> p j e", e=2),
-                in1=b2_cols[:].unsqueeze(2).to_broadcast([P, PAIR_BLOCKS, 2]),
-                op=ALU.mult,
-            )
-            nc.vector.tensor_tensor(
-                out=drive_bias[:], in0=drive_bias[:], in1=vecs[:, 0, :], op=ALU.add
-            )
-            for g in (1, 2, 0):
-                for t0 in range(TILES_PER_HALF, ROW_TILES, 2):
-                    transpose_cat(g, t0)
-            for c in range(0, N_COLS, 2):
-                sigmoids(terms, 0, c)
-                sigmoids(terms, 0, c + 1)
-                self_gain(0, c)
-                self_gain(0, c + 1)
+            regroup_w1(2, 0)
+            regroup_w1(2, 1)
+            widen_max_cond()
+            widen_vecs()
+            quantise_w1(2, 0)
+            make_inv_cap()
+            quantise_w1(2, 1)
+            make_neg_gain()
+            quantise_cat(0, 0)
+            make_drive_gain()
 
-            for g2 in range(PASSES_2):
-                for t in range(TILES_PER_HALF):
-                    first_product(g2, t)
-                    add_b1(g2, t)
-                quantise_h(g2, 0)
-            quantise_w2()
+            c = 5
+            for t0 in (4, 6):
+                for g in (1, 2):
+                    transpose_cat(g, t0)
+                    copy_cat(g, t0)
+                    if c < N_COLS:
+                        sigmoids(0, c)
+                        c += 1
+            for c in range(N_COLS):
+                self_gain(0, c)
+
+            ahead = 3
+            for unit in units[0][:ahead]:
+                first_product(*unit)
+            regroup_w2(0)
+            start_drive_bias()
+            regroup_w2(1)
+            finish_drive_bias()
+            for i, unit in enumerate(units[0]):
+                add_b1(*unit)
+                if i + ahead < len(units[0]):
+                    first_product(*units[0][i + ahead])
+                if i == 1:
+                    quantise_w2()
+                if i == TILES_PER_HALF:
+                    quantise_h(0, 0)
+            for t0 in (4, 6):
+                transpose_cat(0, t0)
+                copy_cat(0, t0)
+            partner_gain(0, 0)
+            quantise_h(1, 0)
 
         late = ctx.enter_context(tc.tile_pool(name="late", bufs=1))
-        row_pool = ctx.enter_context(tc.tile_pool(name="row_pool", bufs=2))
+        row_pool = ctx.enter_context(tc.tile_pool(name="row_pool", bufs=3))
         unused_pool = ctx.enter_context(tc.tile_pool(name="unused_pool", bufs=4))
+        out_rows = out.rearrange("(p t) s -> p t s", t=ROW_TILES)
 
+        pre_banks = {}
         drive = {}
 
         def second_product(h, jb):
@@ -431,12 +482,15 @@ def tile_memorylayercell_pa_kernel(
                     start=(g2 == 0),
                     stop=(g2 == PASSES_2 - 1),
                 )
+            pre_banks[h, jb] = bank
+
+        def scale_drive(h, jb):
             for e in range(2):
                 c = 2 * jb + e
                 drive[h, c] = late.tile([P, HALF], F32, name="drive_%d_%d" % (h, c))
                 nc.scalar.activation(
                     out=drive[h, c][:],
-                    in_=bank[:],
+                    in_=pre_banks[h, jb][:],
                     func=FUNC.Identity,
                     scale=drive_gain[:, c : c + 1],
                     bias=drive_bias[:, c : c + 1],
@@ -469,47 +523,55 @@ def tile_memorylayercell_pa_kernel(
                         )
                 x_banks[t, k] = bank
 
-        def row_mean(t):
-            neg_mean_parts = small.tile([P, 2], F32, name="neg_mean_parts")
-            for k in range(2):
-                unused = unused_pool.tile([P, BANK], BF16, name="unused")
-                nc.scalar.activation(
-                    out=unused[:],
-                    in_=x_banks[t, k][:],
-                    func=FUNC.Identity,
-                    scale=-1.0 / CELLS,
-                    accum_out=neg_mean_parts[:, k : k + 1],
-                )
+        mean_parts, square_parts, part_eps = {}, {}, {}
+
+        def sum_row(t, k):
+            if k == 0:
+                mean_parts[t] = small.tile([P, 2], F32, name="mean_parts")
+            unused = unused_pool.tile([P, BANK], BF16, name="unused")
+            nc.scalar.activation(
+                out=unused[:],
+                in_=x_banks[t, k][:],
+                func=FUNC.Identity,
+                scale=-1.0 / CELLS,
+                accum_out=mean_parts[t][:, k : k + 1],
+            )
+
+        def make_neg_mean(t):
             neg_mean[t] = small.tile([P, 1], F32, name="neg_mean")
             nc.scalar.activation(
                 out=neg_mean[t][:],
-                in_=neg_mean_parts[:, 0:1],
+                in_=mean_parts[t][:, 0:1],
                 func=FUNC.Identity,
-                bias=neg_mean_parts[:, 1:2],
+                bias=mean_parts[t][:, 1:2],
             )
 
-        def row_rstd(t):
-            square_parts = small.tile([P, 2], F32, name="square_parts")
-            for k in range(2):
-                unused = unused_pool.tile([P, BANK], BF16, name="unused")
-                nc.scalar.activation(
-                    out=unused[:],
-                    in_=x_banks[t, k][:],
-                    func=FUNC.Square,
-                    bias=neg_mean[t][:, 0:1],
-                    accum_out=square_parts[:, k : k + 1],
-                )
-            part_eps = small.tile([P, 1], F32, name="part_eps")
+        def sum_squares(t, k):
+            if k == 0:
+                square_parts[t] = small.tile([P, 2], F32, name="square_parts")
+            unused = unused_pool.tile([P, BANK], BF16, name="unused")
             nc.scalar.activation(
-                out=part_eps[:], in_=square_parts[:, 1:2], func=FUNC.Identity, scale=1.0 / CELLS, bias=EPS
+                out=unused[:],
+                in_=x_banks[t, k][:],
+                func=FUNC.Square,
+                bias=neg_mean[t][:, 0:1],
+                accum_out=square_parts[t][:, k : k + 1],
             )
+
+        def make_part_eps(t):
+            part_eps[t] = small.tile([P, 1], F32, name="part_eps")
+            nc.scalar.activation(
+                out=part_eps[t][:], in_=square_parts[t][:, 1:2], func=FUNC.Identity, scale=1.0 / CELLS, bias=EPS
+            )
+
+        def make_rstd(t):
             rstd[t] = small.tile([P, 1], F32, name="rstd")
             nc.scalar.activation(
                 out=rstd[t][:],
-                in_=square_parts[:, 0:1],
+                in_=square_parts[t][:, 0:1],
                 func=FUNC.Abs_reciprocal_sqrt,
                 scale=1.0 / CELLS,
-                bias=part_eps[:, 0:1],
+                bias=part_eps[t][:, 0:1],
             )
 
         def centre(t):
@@ -539,37 +601,71 @@ def tile_memorylayercell_pa_kernel(
 
         for jb in range(PAIR_BLOCKS):
             second_product(0, jb)
-        for g in (1, 2, 0):
-            quantise_cat(g, 1)
-        for c in range(N_COLS):
-            partner_gain(0, c)
-            product(0, c, 0)
-            product(0, c, 1)
+        quantise_cat(1, 1)
+        quantise_cat(2, 1)
+        lag = 2
+        for c in range(N_COLS + lag):
+            if c < N_COLS:
+                products(0, c)
+            if c < PAIR_BLOCKS:
+                scale_drive(0, c)
+            if c == 0:
+                quantise_cat(0, 1)
+            if c == lag - 1:
+                for unit in units[1][:ahead]:
+                    first_product(*unit)
+            if c >= lag:
+                i = c - lag
+                add_b1(*units[1][i])
+                if i + ahead < len(units[1]):
+                    first_product(*units[1][i + ahead])
+                if i == TILES_PER_HALF + 1:
+                    quantise_h(0, 1)
         for c in range(0, N_COLS, 2):
-            sigmoids(terms, 1, c)
-            sigmoids(terms, 1, c + 1)
+            sigmoids(1, c)
+            sigmoids(1, c + 1)
             self_gain(1, c)
             self_gain(1, c + 1)
-        for g2 in range(PASSES_2):
-            for t in range(TILES_PER_HALF, ROW_TILES):
-                first_product(g2, t)
-                add_b1(g2, t)
-            quantise_h(g2, 1)
-        for jb in range(PAIR_BLOCKS):
-            second_product(1, jb)
+        partner_gain(1, 0)
+        quantise_h(1, 1)
+
         row_layout(0)
-        row_mean(0)
+        for k in range(2):
+            sum_row(0, k)
+        make_neg_mean(0)
         for t in range(ROW_TILES):
-            if t < TILES_PER_HALF:
-                for c in (2 * t, 2 * t + 1):
-                    partner_gain(1, c)
-                    product(1, c, 0)
-                    product(1, c, 1)
-            if t + 1 < ROW_TILES:
+            products_first = t + 1 == TILES_PER_HALF
+            more = t + 1 < ROW_TILES and not products_first
+            if more:
                 row_layout(t + 1)
-                row_mean(t + 1)
-            row_rstd(t)
-            centre(t)
+            if t == 0:
+                for jb in range(PAIR_BLOCKS):
+                    second_product(1, jb)
+            for k in range(2):
+                if more:
+                    sum_row(t + 1, k)
+                if k == 0 and t > 0:
+                    make_rstd(t - 1)
+                sum_squares(t, k)
+            if more:
+                make_neg_mean(t + 1)
+            make_part_eps(t)
+            if t < TILES_PER_HALF:
+                products(1, 2 * t)
+                products(1, 2 * t + 1)
+            if t < 2:
+                scale_drive(1, 2 * t)
+                scale_drive(1, 2 * t + 1)
             if t > 0:
-                store_rows(t - 1)
+                centre(t - 1)
+            if products_first:
+                row_layout(t + 1)
+                for k in range(2):
+                    sum_row(t + 1, k)
+                make_neg_mean(t + 1)
+            if t > 1:
+                store_rows(t - 2)
+        make_rstd(ROW_TILES - 1)
+        centre(ROW_TILES - 1)
+        store_rows(ROW_TILES - 2)
         store_rows(ROW_TILES - 1)

@@ -64,15 +64,7 @@ def tile_memorylayercell_pa_kernel(
             return psum.tile([P, BANK], F32, name=label, tag="bank")
 
         first_rows = consts.tile([P, 8 * P], BF16)
-        for a, mat in enumerate((mean_conductance_potential, std_conductance)):
-            for k in range(2):
-                first = 64 * a + 32 * k
-                nc.scalar.dma_start(
-                    out=first_rows[first : first + 32, :],
-                    in_=mat[4 * P * k : 4 * P * (k + 1), :]
-                    .rearrange("c s -> (c s)")
-                    .partition_broadcast(32),
-                )
+        nc.gpsimd.memset(first_rows[:].bitcast(F32), 0.0)
         later_rows = consts.tile([P, 8 * P], BF16)
         ident_f32 = consts.tile([P, P], F32)
         make_identity(nc, ident_f32[:])
@@ -113,7 +105,7 @@ def tile_memorylayercell_pa_kernel(
         def widen_first():
             nc.vector.tensor_copy(
                 out=mats[:].rearrange("p a (k q) s -> p (a k) q s", k=2),
-                in_=bank_halves("first_bank", 4)[:, 0 : 4 * 32 : 32, :, :],
+                in_=bank_halves("first_bank", 4)[:, 0:4, :, :],
             )
 
         def make_shift():
@@ -296,6 +288,11 @@ def tile_memorylayercell_pa_kernel(
 
             w1_raw = {}
             load_w1(0)
+            for a, mat in enumerate((mean_conductance_potential, std_conductance)):
+                nc.sync.dma_start(
+                    out=first_rows[2 * a : 2 * a + 2, :],
+                    in_=mat.rearrange("(k c) s -> k (c s)", k=2),
+                )
             load_rows(states_nat, states_rows, 0)
             load_w1(1)
             load_rows(inputs_nat, inputs_rows, 0)

@@ -53,7 +53,6 @@ def tile_memorylayercell_pa_kernel(
 ):
     nc = tc.nc
     with ExitStack() as ctx:
-        ctx.enter_context(tc.manual_schedule())
         consts = ctx.enter_context(tc.tile_pool(name="consts", bufs=1))
         keep = ctx.enter_context(tc.tile_pool(name="keep", bufs=1))
         terms = ctx.enter_context(tc.tile_pool(name="terms", bufs=1))
@@ -293,10 +292,10 @@ def tile_memorylayercell_pa_kernel(
                     out=first_rows[2 * a : 2 * a + 2, :],
                     in_=mat.rearrange("(k c) s -> k (c s)", k=2),
                 )
-            load_rows(states_nat, states_rows, 0)
             load_w1(1)
-            load_rows(inputs_nat, inputs_rows, 0)
+            load_rows(states_nat, states_rows, 0)
             load_w1(2)
+            load_rows(inputs_nat, inputs_rows, 0)
             nc.sync.dma_start(
                 out=later_rows[0:2, :], in_=max_conductance.rearrange("(k c) s -> k (c s)", k=2)
             )
@@ -342,12 +341,13 @@ def tile_memorylayercell_pa_kernel(
             w1_grouped = {}
 
             def regroup_w1(g, g2):
+                copy = nc.scalar.copy if (g, g2) == (0, 1) else nc.vector.tensor_copy
                 if g2 == 0:
                     w1_grouped[g] = w_grouped_pool.tile(
                         [P, CELLS, PACK], BF16, name="w1_grouped", tag="w_grouped", align_bytes=64
                     )
                 cols = slice(K_PASS * g2, K_PASS * (g2 + 1))
-                nc.vector.tensor_copy(
+                copy(
                     out=w1_grouped[g][:, cols, :].rearrange("p (i m) t -> p m t i", i=PACK),
                     in_=w1_raw[g][:, :, cols].rearrange("p t (m i) -> p m t i", i=PACK),
                 )
@@ -381,28 +381,30 @@ def tile_memorylayercell_pa_kernel(
                     in_=w2_grouped[0][:].rearrange("p g c t -> p (g c t)"),
                 )
 
-            for t0 in (0, 2):
-                for g in (1, 2):
-                    transpose_cat(g, t0)
-                    copy_cat(g, t0)
-            for g2 in range(PASSES_2):
-                regroup_w1(0, g2)
-            for g2 in range(PASSES_2):
-                quantise_w1(0, g2)
+            def cat(g, t0):
+                transpose_cat(g, t0)
+                copy_cat(g, t0)
+
+            regroup_w1(0, 0)
+            regroup_w1(0, 1)
+            for g in (1, 2):
+                cat(g, 0)
             transpose_cells(first_rows[:].bitcast(F32), "first_bank")
-            for t0 in (0, 2):
-                transpose_cat(0, t0)
-                copy_cat(0, t0)
-            regroup_w1(1, 0)
-            regroup_w1(1, 1)
             widen_first()
-            quantise_w1(1, 0)
             make_shift()
-            quantise_w1(1, 1)
-            quantise_cat(1, 0)
-            quantise_cat(2, 0)
-            for c in range(5):
-                sigmoids(0, c)
+            for g in (1, 2):
+                cat(g, 2)
+            for t0 in (0, 2):
+                cat(0, t0)
+            for g in range(PASSES_1):
+                if g > 0:
+                    for g2 in range(PASSES_2):
+                        regroup_w1(g, g2)
+                for g2 in range(PASSES_2):
+                    quantise_w1(g, g2)
+                if g == 1:
+                    for g_cat in (1, 2, 0):
+                        quantise_cat(g_cat, 0)
 
             later_words = later_rows[:].bitcast(F32)
             transpose_cells(later_words, "gain_bank")
@@ -414,48 +416,30 @@ def tile_memorylayercell_pa_kernel(
             nc.tensor.transpose(
                 const_banks["vec_bank"][:, 2 * P : 3 * P], later_words[:, 0:P], ident_f32[:]
             )
-            regroup_w1(2, 0)
-            regroup_w1(2, 1)
             widen_max_cond()
             widen_vecs()
-            quantise_w1(2, 0)
             make_inv_cap()
-            quantise_w1(2, 1)
             make_neg_gain()
-            quantise_cat(0, 0)
             make_drive_gain()
-
-            c = 5
-            for t0 in (4, 6):
-                for g in (1, 2):
-                    transpose_cat(g, t0)
-                    copy_cat(g, t0)
-                    if c < N_COLS:
-                        sigmoids(0, c)
-                        c += 1
-            for c in range(N_COLS):
-                self_gain(0, c)
-
-            ahead = 3
-            for unit in units[0][:ahead]:
-                first_product(*unit)
-            regroup_w2(0)
             start_drive_bias()
-            regroup_w2(1)
             finish_drive_bias()
-            for i, unit in enumerate(units[0]):
+
+            for g in (1, 2, 0):
+                for t0 in (4, 6):
+                    cat(g, t0)
+            for c in range(0, N_COLS, 2):
+                sigmoids(0, c)
+                sigmoids(0, c + 1)
+                self_gain(0, c)
+                self_gain(0, c + 1)
+            for unit in units[0]:
+                first_product(*unit)
                 add_b1(*unit)
-                if i + ahead < len(units[0]):
-                    first_product(*units[0][i + ahead])
-                if i == 1:
-                    quantise_w2()
-                if i == TILES_PER_HALF:
-                    quantise_h(0, 0)
-            for t0 in (4, 6):
-                transpose_cat(0, t0)
-                copy_cat(0, t0)
-            partner_gain(0, 0)
-            quantise_h(1, 0)
+                if unit[1] == TILES_PER_HALF - 1:
+                    quantise_h(unit[0], 0)
+            regroup_w2(0)
+            regroup_w2(1)
+            quantise_w2()
 
         late = ctx.enter_context(tc.tile_pool(name="late", bufs=1))
         row_pool = ctx.enter_context(tc.tile_pool(name="row_pool", bufs=3))
@@ -598,71 +582,48 @@ def tile_memorylayercell_pa_kernel(
 
         for jb in range(PAIR_BLOCKS):
             second_product(0, jb)
-        quantise_cat(1, 1)
-        quantise_cat(2, 1)
-        lag = 2
-        for c in range(N_COLS + lag):
-            if c < N_COLS:
-                products(0, c)
-            if c < PAIR_BLOCKS:
-                scale_drive(0, c)
-            if c == 0:
-                quantise_cat(0, 1)
-            if c == lag - 1:
-                for unit in units[1][:ahead]:
-                    first_product(*unit)
-            if c >= lag:
-                i = c - lag
-                add_b1(*units[1][i])
-                if i + ahead < len(units[1]):
-                    first_product(*units[1][i + ahead])
-                if i == TILES_PER_HALF + 1:
-                    quantise_h(0, 1)
+            scale_drive(0, jb)
+        for g in (1, 2, 0):
+            quantise_cat(g, 1)
+        partner_gain(0, 0)
+        for c in range(N_COLS):
+            products(0, c)
         for c in range(0, N_COLS, 2):
             sigmoids(1, c)
             sigmoids(1, c + 1)
             self_gain(1, c)
             self_gain(1, c + 1)
-        partner_gain(1, 0)
-        quantise_h(1, 1)
+        for unit in units[1]:
+            first_product(*unit)
+            add_b1(*unit)
+            if unit[1] == ROW_TILES - 1:
+                quantise_h(unit[0], 1)
+        for jb in range(PAIR_BLOCKS):
+            second_product(1, jb)
+            scale_drive(1, jb)
 
-        row_layout(0)
-        for k in range(2):
-            sum_row(0, k)
-        make_neg_mean(0)
-        for t in range(ROW_TILES):
-            products_first = t + 1 == TILES_PER_HALF
-            more = t + 1 < ROW_TILES and not products_first
-            if more:
-                row_layout(t + 1)
-            if t == 0:
-                for jb in range(PAIR_BLOCKS):
-                    second_product(1, jb)
+        def row_mean(t):
+            row_layout(t)
             for k in range(2):
-                if more:
-                    sum_row(t + 1, k)
-                if k == 0 and t > 0:
-                    make_rstd(t - 1)
+                sum_row(t, k)
+            make_neg_mean(t)
+
+        def row_rstd(t):
+            for k in range(2):
                 sum_squares(t, k)
-            if more:
-                make_neg_mean(t + 1)
             make_part_eps(t)
+            make_rstd(t)
+
+        row_mean(0)
+        partner_gain(1, 0)
+        for t in range(ROW_TILES):
             if t < TILES_PER_HALF:
                 products(1, 2 * t)
                 products(1, 2 * t + 1)
-            if t < 2:
-                scale_drive(1, 2 * t)
-                scale_drive(1, 2 * t + 1)
+            if t + 1 < ROW_TILES:
+                row_mean(t + 1)
+            row_rstd(t)
+            centre(t)
             if t > 0:
-                centre(t - 1)
-            if products_first:
-                row_layout(t + 1)
-                for k in range(2):
-                    sum_row(t + 1, k)
-                make_neg_mean(t + 1)
-            if t > 1:
-                store_rows(t - 2)
-        make_rstd(ROW_TILES - 1)
-        centre(ROW_TILES - 1)
-        store_rows(ROW_TILES - 2)
+                store_rows(t - 1)
         store_rows(ROW_TILES - 1)

@@ -292,8 +292,8 @@ def tile_memorylayercell_pa_kernel(
                     out=first_rows[2 * a : 2 * a + 2, :],
                     in_=mat.rearrange("(k c) s -> k (c s)", k=2),
                 )
-            load_w1(1)
             load_rows(states_nat, states_rows, 0)
+            load_w1(1)
             load_w1(2)
             load_rows(inputs_nat, inputs_rows, 0)
             nc.sync.dma_start(
@@ -341,13 +341,12 @@ def tile_memorylayercell_pa_kernel(
             w1_grouped = {}
 
             def regroup_w1(g, g2):
-                copy = nc.scalar.copy if (g, g2) == (0, 1) else nc.vector.tensor_copy
                 if g2 == 0:
                     w1_grouped[g] = w_grouped_pool.tile(
                         [P, CELLS, PACK], BF16, name="w1_grouped", tag="w_grouped", align_bytes=64
                     )
                 cols = slice(K_PASS * g2, K_PASS * (g2 + 1))
-                copy(
+                nc.vector.tensor_copy(
                     out=w1_grouped[g][:, cols, :].rearrange("p (i m) t -> p m t i", i=PACK),
                     in_=w1_raw[g][:, :, cols].rearrange("p t (m i) -> p m t i", i=PACK),
                 )

from contextlib import ExitStack

import concourse.mybir as mybir
from concourse.masks import make_identity

F32 = mybir.dt.float32
BF16 = mybir.dt.bfloat16
U32 = mybir.dt.uint32
U8 = mybir.dt.uint8
FP8X4 = mybir.dt.float8_e4m3fn_x4
ALU = mybir.AluOpType
FUNC = mybir.ActivationFunctionType

P = 128
PACK = 4
K_PASS = P * PACK
BANK = 512

ROWS, D_IN, CELLS = 1024, 512, 1024
PAIRS = CELLS // 2
K1 = D_IN + CELLS
EPS = 1e-6

ROW_TILES = ROWS // P
HALF = ROWS // 2
HALVES = 2
TILES_PER_HALF = HALF // P
PASSES_1 = K1 // K_PASS
PASSES_2 = CELLS // K_PASS
PAIR_BLOCKS = PAIRS // P
N_COLS = 2 * PAIR_BLOCKS

FLOPS = 2 * ROWS * K1 * CELLS + 2 * ROWS * CELLS * PAIRS


def tile_memorylayercell_pa_kernel(
    tc,
    inputs,
    states,
    W1,
    b1,
    W2,
    b2,
    excitatory_potential,
    inhibitory_potential,
    capacitance,
    max_conductance,
    mean_conductance_potential,
    std_conductance,
    gamma,
    beta,
    out,
):
    nc = tc.nc
    with ExitStack() as ctx:
        consts = ctx.enter_context(tc.tile_pool(name="consts", bufs=1))
        keep = ctx.enter_context(tc.tile_pool(name="keep", bufs=1))
        terms = ctx.enter_context(tc.tile_pool(name="terms", bufs=1))
        small = ctx.enter_context(tc.tile_pool(name="small", bufs=6))
        psum = ctx.enter_context(tc.psum_pool(name="psum", bufs=8))

        def new_bank(label):
            return psum.tile([P, BANK], F32, name=label, tag="bank")

        first_rows = consts.tile([P, 8 * P], BF16)
        nc.gpsimd.memset(first_rows[:].bitcast(F32), 0.0)
        later_rows = consts.tile([P, 8 * P], BF16)
        ident_f32 = consts.tile([P, P], F32)
        make_identity(nc, ident_f32[:])
        nc.gpsimd.memset(later_rows[:].bitcast(F32), 0.0)
        sign = consts.tile([P, PAIR_BLOCKS, 2], F32)
        nc.gpsimd.memset(sign[:, :, 0], 1.0)
        nc.gpsimd.memset(sign[:, :, 1], -1.0)
        table_probe = consts.tile([P, 1], F32)
        nc.vector.memset(table_probe[:], 0.0)
        nc.scalar.activation(out=table_probe[:], in_=table_probe[:], func=FUNC.Sigmoid)

        mats = consts.tile([P, 2, N_COLS, 2], F32)
        mean_pot = mats[:, 0, :, :]
        slope = mats[:, 1, :, :]
        shift = consts.tile([P, N_COLS, 2], F32)
        max_cond = consts.tile([P, N_COLS, 2], F32)
        vecs = consts.tile([P, 4, N_COLS], F32)
        reversal = vecs[:, 0:2, :]
        b1_cols = vecs[:, 3, :].rearrange("p (g t) -> p g t", g=PASSES_2)
        inv_cap = consts.tile([P, N_COLS], F32)
        neg_gain = consts.tile([P, N_COLS, 2], F32)
        drive_gain = consts.tile([P, N_COLS], F32)
        drive_bias = consts.tile([P, N_COLS], F32)
        const_banks = {}

        def transpose_cells(rows, label):
            const_banks[label] = new_bank(label)
            for q in range(4):
                nc.tensor.transpose(
                    const_banks[label][:, P * q : P * (q + 1)], rows[:, q : 4 * P : 4], ident_f32[:]
                )

        def bank_halves(label, blocks):
            return const_banks[label][:].bitcast(BF16)[:, 0 : 2 * P * blocks].rearrange(
                "p (q r s) -> p r q s", q=blocks, s=2
            )

        def widen_first():
            nc.vector.tensor_copy(
                out=mats[:].rearrange("p a (k q) s -> p (a k) q s", k=2),
                in_=bank_halves("first_bank", 4)[:, 0:4, :, :],
            )

        def make_shift():
            nc.vector.scalar_tensor_tensor(
                out=shift[:], in0=slope, scalar=-1.0, in1=mean_pot, op0=ALU.mult, op1=ALU.mult
            )

        def widen_max_cond():
            nc.vector.tensor_copy(
                out=max_cond[:].rearrange("p (k q) s -> p k q s", k=2),
                in_=bank_halves("gain_bank", 4)[:, 0:2, :, :],
            )

        def widen_vecs():
            nc.vector.tensor_copy(
                out=vecs[:].rearrange("p v (k u e) -> p (v k) u e", k=2, u=2),
                in_=bank_halves("vec_bank", 3)[:, 2:10, 0:2, :],
            )

        def make_inv_cap():
            nc.vector.reciprocal(out=inv_cap[:], in_=vecs[:, 2, :])

        def make_neg_gain():
            nc.vector.scalar_tensor_tensor(
                out=neg_gain[:],
                in0=max_cond[:],
                scalar=-1.0,
                in1=inv_cap[:].unsqueeze(2).to_broadcast([P, N_COLS, 2]),
                op0=ALU.mult,
                op1=ALU.mult,
            )

        def make_drive_gain():
            nc.vector.tensor_mul(
                out=drive_gain[:], in0=inv_cap[:], in1=sign[:].rearrange("p j e -> p (j e)")
            )

        def start_drive_bias():
            b2_pairs = bank_halves("vec_bank", 3)[:, 10:12, 2, :]
            nc.vector.tensor_mul(
                out=drive_bias[:].rearrange("p (k u e) -> p k u e", k=2, u=2),
                in0=drive_gain[:].rearrange("p (k u e) -> p k u e", k=2, u=2),
                in1=b2_pairs.unsqueeze(3).to_broadcast([P, 2, 2, 2]),
            )

        def finish_drive_bias():
            nc.vector.tensor_add(out=drive_bias[:], in0=drive_bias[:], in1=vecs[:, 0, :])

        cat_grouped = keep.tile([P, PASSES_1, ROWS, PACK], BF16, align_bytes=64)
        cat_codes = keep.tile([P, PASSES_1, ROWS], U32, align_bytes=64)
        cat_scales = keep.tile([P, PASSES_1, ROWS], U8, align_bytes=64)
        cat_words = cat_grouped[:].bitcast(F32)
        w1_codes = keep.tile([P, PASSES_1, CELLS], U32, align_bytes=64)
        w1_scales = keep.tile([P, PASSES_1, CELLS], U8, align_bytes=64)
        w2_codes = keep.tile([P, PASSES_2, PAIRS], U32, align_bytes=64)
        w2_scales = keep.tile([P, PASSES_2, PAIRS], U8, align_bytes=64)
        h_grouped = keep.tile([P, PASSES_2, ROWS, PACK], BF16, align_bytes=64)
        h_codes = keep.tile([P, PASSES_2, ROWS], U32, align_bytes=64)
        h_scales = keep.tile([P, PASSES_2, ROWS], U8, align_bytes=64)
        gamma_rows = consts.tile([P, CELLS], BF16)
        beta_rows = consts.tile([P, CELLS], BF16)

        h_banks = {}

        def quantise_cat(g, h):
            rows = slice(HALF * h, HALF * (h + 1))
            nc.vector.quantize_mx(
                out=cat_codes[:, g, rows].bitcast(FP8X4),
                scales=cat_scales[:, g, rows],
                in_=cat_grouped[:, g, rows, :].rearrange("p r t -> p (r t)"),
            )

        def first_product(g2, t):
            rows = slice(P * t, P * (t + 1))
            bank = new_bank("h_bank")
            for t4 in range(PACK):
                cols = slice(K_PASS * g2 + P * t4, K_PASS * g2 + P * (t4 + 1))
                for g in range(PASSES_1):
                    nc.tensor.matmul_mx(
                        out=bank[:, P * t4 : P * (t4 + 1)],
                        lhsT=w1_codes[:, g, cols].bitcast(FP8X4),
                        lhsT_scale=w1_scales[:, g, cols],
                        rhs=cat_codes[:, g, rows].bitcast(FP8X4),
                        rhs_scale=cat_scales[:, g, rows],
                        start=(g == 0),
                        stop=(g == PASSES_1 - 1),
                    )
            h_banks[g2, t] = bank

        def add_b1(g2, t):
            nc.vector.tensor_tensor(
                out=h_grouped[:, g2, P * t : P * (t + 1), :],
                in0=h_banks[g2, t][:].rearrange("p (t r) -> p r t", t=PACK),
                in1=b1_cols[:, g2, :].unsqueeze(1).to_broadcast([P, P, PACK]),
                op=ALU.add,
            )

        def quantise_h(g2, h):
            rows = slice(HALF * h, HALF * (h + 1))
            nc.vector.quantize_mx(
                out=h_codes[:, g2, rows].bitcast(FP8X4),
                scales=h_scales[:, g2, rows],
                in_=h_grouped[:, g2, rows, :].rearrange("p r t -> p (r t)"),
            )

        terms_of = {}

        def sigmoids(h, c):
            rows = slice(HALF * h, HALF * (h + 1))
            g, b = 1 + c // PACK, c % PACK
            own = terms.tile([P, HALF], F32, name="self_%d_%d" % (h, c))
            other = terms.tile([P, HALF], F32, name="partner_%d_%d" % (h, c))
            partner = b + 1 - 2 * (b % 2)
            for syn, dst, value in ((1, other, partner), (0, own, b)):
                nc.scalar.activation(
                    out=dst[:],
                    in_=cat_grouped[:, g, rows, value],
                    func=FUNC.Sigmoid,
                    scale=slope[:, c : c + 1, syn],
                    bias=shift[:, c : c + 1, syn],
                )
            terms_of[h, c] = (own, other)

        def self_gain(h, c):
            own = terms_of[h, c][0]
            nc.scalar.activation(
                out=own[:], in_=own[:], func=FUNC.Identity, scale=neg_gain[:, c : c + 1, 0], bias=1.0
            )

        def partner_gain(h, c):
            other = terms_of[h, c][1]
            nc.vector.tensor_scalar_mul(out=other[:], in0=other[:], scalar1=neg_gain[:, c : c + 1, 1])

        def product(h, c, syn):
            dst = terms_of[h, c][syn]
            rows = slice(HALF * h, HALF * (h + 1))
            nc.vector.scalar_tensor_tensor(
                out=dst[:],
                in0=cat_grouped[:, 1 + c // PACK, rows, c % PACK],
                scalar=reversal[:, syn, c : c + 1],
                in1=dst[:],
                op0=ALU.subtract,
                op1=ALU.mult,
            )

        def products(h, c):
            if c + 1 < N_COLS:
                partner_gain(h, c + 1)
            product(h, c, 1)
            product(h, c, 0)

        units = {
            h: [(g2, TILES_PER_HALF * h + i) for g2 in range(PASSES_2) for i in range(TILES_PER_HALF)]
            for h in range(HALVES)
        }

        with (
            tc.tile_pool(name="natural", bufs=1) as natural,
            tc.tile_pool(name="w_raw", bufs=1) as w_raw_pool,
            tc.tile_pool(name="w_grouped", bufs=2) as w_grouped_pool,
        ):
            states_rows = states.rearrange("(p t) s -> p t s", t=ROW_TILES)
            inputs_rows = inputs.rearrange("(p t) s -> p t s", t=ROW_TILES)
            states_nat = natural.tile([P, ROW_TILES, CELLS], BF16)
            inputs_nat = natural.tile([P, ROW_TILES, D_IN], BF16)
            inputs_words = inputs_nat[:].bitcast(F32)
            states_words = states_nat[:].bitcast(F32)

            def load_rows(nat, rows, h):
                tiles = slice(TILES_PER_HALF * h, TILES_PER_HALF * (h + 1))
                nc.sync.dma_start(out=nat[:, tiles, :], in_=rows[:, tiles, :])

            def load_w1(g):
                raw = w_raw_pool.tile([P, PACK, CELLS], BF16, name="w1_raw_%d" % g)
                nc.sync.dma_start(
                    out=raw[:],
                    in_=W1[K_PASS * g : K_PASS * (g + 1), :].rearrange("(q t) s -> q t s", t=PACK),
                )
                w1_raw[g] = raw

            w1_raw = {}
            load_w1(0)
            for a, mat in enumerate((mean_conductance_potential, std_conductance)):
                nc.sync.dma_start(
                    out=first_rows[2 * a : 2 * a + 2, :],
                    in_=mat.rearrange("(k c) s -> k (c s)", k=2),
                )
            load_rows(states_nat, states_rows, 0)
            load_w1(1)
            load_w1(2)
            load_rows(inputs_nat, inputs_rows, 0)
            nc.sync.dma_start(
                out=later_rows[0:2, :], in_=max_conductance.rearrange("(k c) s -> k (c s)", k=2)
            )
            for v, vec in enumerate((excitatory_potential, inhibitory_potential, capacitance, b1)):
                nc.sync.dma_start(
                    out=later_rows[2 + 2 * v : 4 + 2 * v, 0 : 4 * P],
                    in_=vec.rearrange("(k c) -> k c", k=2),
                )
            nc.sync.dma_start(
                out=later_rows[10:12, 0 : 2 * P], in_=b2.rearrange("(k c) -> k c", k=2)
            )
            load_rows(states_nat, states_rows, 1)
            w2_raw = w_raw_pool.tile([P, PASSES_2, PACK, PAIRS], BF16, name="w2_raw")
            nc.sync.dma_start(
                out=w2_raw[:], in_=W2.rearrange("(g p t) n -> p g t n", g=PASSES_2, t=PACK)
            )
            load_rows(inputs_nat, inputs_rows, 1)
            nc.sync.dma_start(out=gamma_rows[:], in_=gamma.partition_broadcast(P))
            nc.sync.dma_start(out=beta_rows[:], in_=beta.partition_broadcast(P))

            cat_banks = {}

            def transpose_cat(g, t0):
                bank = new_bank("cat_bank")
                for u in range(2):
                    for i in range(2):
                        if g == 0:
                            words = inputs_words[:, t0 + i, u : 2 * P : 2]
                        else:
                            first = 2 * P * (g - 1)
                            words = states_words[:, t0 + i, first + u : first + 2 * P : 2]
                        nc.tensor.transpose(
                            bank[:, P * (2 * u + i) : P * (2 * u + i + 1)], words, ident_f32[:]
                        )
                cat_banks[g, t0] = bank

            def copy_cat(g, t0):
                nc.scalar.copy(
                    out=cat_words[:, g, P * t0 : P * (t0 + 2), :],
                    in_=cat_banks[g, t0][:].rearrange("p (u r) -> p r u", u=2),
                )

            w1_grouped = {}

            def regroup_w1(g, g2):
                if g2 == 0:
                    w1_grouped[g] = w_grouped_pool.tile(
                        [P, CELLS, PACK], BF16, name="w1_grouped", tag="w_grouped", align_bytes=64
                    )
                cols = slice(K_PASS * g2, K_PASS * (g2 + 1))
                nc.vector.tensor_copy(
                    out=w1_grouped[g][:, cols, :].rearrange("p (i m) t -> p m t i", i=PACK),
                    in_=w1_raw[g][:, :, cols].rearrange("p t (m i) -> p m t i", i=PACK),
                )

            def quantise_w1(g, g2):
                cols = slice(K_PASS * g2, K_PASS * (g2 + 1))
                nc.vector.quantize_mx(
                    out=w1_codes[:, g, cols].bitcast(FP8X4),
                    scales=w1_scales[:, g, cols],
                    in_=w1_grouped[g][:, cols, :].rearrange("p c t -> p (c t)"),
                )

            w2_grouped = []

            def regroup_w2(g):
                if g == 0:
                    w2_grouped.append(
                        w_grouped_pool.tile(
                            [P, PASSES_2, PAIRS, PACK], BF16, name="w2_grouped", tag="w_grouped", align_bytes=64
                        )
                    )
                nc.vector.tensor_copy(
                    out=w2_grouped[0][:, g, :, :].rearrange("p (k u m) t -> p k m t u", k=2, u=2),
                    in_=w2_raw[:, g, :, :].rearrange("p t (k m u) -> p k m t u", k=2, u=2),
                )

            def quantise_w2():
                nc.vector.quantize_mx(
                    out=w2_codes[:].rearrange("p g c -> p (g c)").bitcast(FP8X4),
                    scales=w2_scales[:].rearrange("p g c -> p (g c)"),
                    in_=w2_grouped[0][:].rearrange("p g c t -> p (g c t)"),
                )

            def cat(g, t0):
                transpose_cat(g, t0)
                copy_cat(g, t0)

            regroup_w1(0, 0)
            regroup_w1(0, 1)
            for g in (1, 2):
                cat(g, 0)
            transpose_cells(first_rows[:].bitcast(F32), "first_bank")
            widen_first()
            make_shift()
            for g in (1, 2):
                cat(g, 2)
            for t0 in (0, 2):
                cat(0, t0)
            for g in range(PASSES_1):
                if g > 0:
                    for g2 in range(PASSES_2):
                        regroup_w1(g, g2)
                for g2 in range(PASSES_2):
                    quantise_w1(g, g2)
                if g == 1:
                    for g_cat in (1, 2, 0):
                        quantise_cat(g_cat, 0)

            later_words = later_rows[:].bitcast(F32)
            transpose_cells(later_words, "gain_bank")
            const_banks["vec_bank"] = new_bank("vec_bank")
            for u in range(2):
                nc.tensor.transpose(
                    const_banks["vec_bank"][:, P * u : P * (u + 1)], later_words[:, u : 2 * P : 2], ident_f32[:]
                )
            nc.tensor.transpose(
                const_banks["vec_bank"][:, 2 * P : 3 * P], later_words[:, 0:P], ident_f32[:]
            )
            widen_max_cond()
            widen_vecs()
            make_inv_cap()
            make_neg_gain()
            make_drive_gain()
            start_drive_bias()
            finish_drive_bias()

            for g in (1, 2, 0):
                for t0 in (4, 6):
                    cat(g, t0)
            for c in range(0, N_COLS, 2):
                sigmoids(0, c)
                sigmoids(0, c + 1)
                self_gain(0, c)
                self_gain(0, c + 1)
            for unit in units[0]:
                first_product(*unit)
                add_b1(*unit)
                if unit[1] == TILES_PER_HALF - 1:
                    quantise_h(unit[0], 0)
            regroup_w2(0)
            regroup_w2(1)
            quantise_w2()

        late = ctx.enter_context(tc.tile_pool(name="late", bufs=1))
        row_pool = ctx.enter_context(tc.tile_pool(name="row_pool", bufs=3))
        unused_pool = ctx.enter_context(tc.tile_pool(name="unused_pool", bufs=4))
        out_rows = out.rearrange("(p t) s -> p t s", t=ROW_TILES)

        pre_banks = {}
        drive = {}

        def second_product(h, jb):
            rows = slice(HALF * h, HALF * (h + 1))
            cols = slice(P * jb, P * (jb + 1))
            bank = new_bank("pre_bank")
            for g2 in range(PASSES_2):
                nc.tensor.matmul_mx(
                    out=bank[:],
                    lhsT=w2_codes[:, g2, cols].bitcast(FP8X4),
                    lhsT_scale=w2_scales[:, g2, cols],
                    rhs=h_codes[:, g2, rows].bitcast(FP8X4),
                    rhs_scale=h_scales[:, g2, rows],
                    start=(g2 == 0),
                    stop=(g2 == PASSES_2 - 1),
                )
            pre_banks[h, jb] = bank

        def scale_drive(h, jb):
            for e in range(2):
                c = 2 * jb + e
                drive[h, c] = late.tile([P, HALF], F32, name="drive_%d_%d" % (h, c))
                nc.scalar.activation(
                    out=drive[h, c][:],
                    in_=pre_banks[h, jb][:],
                    func=FUNC.Identity,
                    scale=drive_gain[:, c : c + 1],
                    bias=drive_bias[:, c : c + 1],
                )

        x_banks, neg_mean, rstd, centred = {}, {}, {}, {}

        def row_layout(t):
            h, lanes = t // TILES_PER_HALF, slice(P * (t % TILES_PER_HALF), P * (t % TILES_PER_HALF + 1))
            for k in range(2):
                bank = new_bank("x_bank")
                nc.tensor.matmul(
                    out=bank[:],
                    lhsT=first_rows[:, 0:P],
                    rhs=first_rows[:, 0:BANK],
                    start=True,
                    stop=True,
                )
                for b in range(PACK):
                    c = PACK * k + b
                    parts = terms_of[h, c] + (drive[h, c],)
                    for i, part in enumerate(parts):
                        nc.tensor.matmul(
                            out=bank[:, P * b : P * (b + 1)],
                            lhsT=part[:, lanes],
                            rhs=ident_f32[:],
                            is_transpose=True,
                            start=(i == 0),
                            stop=(i == len(parts) - 1),
                        )
                x_banks[t, k] = bank

        mean_parts, square_parts, part_eps = {}, {}, {}

        def sum_row(t, k):
            if k == 0:
                mean_parts[t] = small.tile([P, 2], F32, name="mean_parts")
            unused = unused_pool.tile([P, BANK], BF16, name="unused")
            nc.scalar.activation(
                out=unused[:],
                in_=x_banks[t, k][:],
                func=FUNC.Identity,
                scale=-1.0 / CELLS,
                accum_out=mean_parts[t][:, k : k + 1],
            )

        def make_neg_mean(t):
            neg_mean[t] = small.tile([P, 1], F32, name="neg_mean")
            nc.scalar.activation(
                out=neg_mean[t][:],
                in_=mean_parts[t][:, 0:1],
                func=FUNC.Identity,
                bias=mean_parts[t][:, 1:2],
            )

        def sum_squares(t, k):
            if k == 0:
                square_parts[t] = small.tile([P, 2], F32, name="square_parts")
            unused = unused_pool.tile([P, BANK], BF16, name="unused")
            nc.scalar.activation(
                out=unused[:],
                in_=x_banks[t, k][:],
                func=FUNC.Square,
                bias=neg_mean[t][:, 0:1],
                accum_out=square_parts[t][:, k : k + 1],
            )

        def make_part_eps(t):
            part_eps[t] = small.tile([P, 1], F32, name="part_eps")
            nc.scalar.activation(
                out=part_eps[t][:], in_=square_parts[t][:, 1:2], func=FUNC.Identity, scale=1.0 / CELLS, bias=EPS
            )

        def make_rstd(t):
            rstd[t] = small.tile([P, 1], F32, name="rstd")
            nc.scalar.activation(
                out=rstd[t][:],
                in_=square_parts[t][:, 0:1],
                func=FUNC.Abs_reciprocal_sqrt,
                scale=1.0 / CELLS,
                bias=part_eps[t][:, 0:1],
            )

        def centre(t):
            centred[t] = row_pool.tile([P, CELLS], F32, name="centred")
            for k in range(2):
                cells = slice(BANK * k, BANK * (k + 1))
                nc.vector.scalar_tensor_tensor(
                    out=centred[t][:, cells].rearrange("p (m b) -> p m b", b=PACK),
                    in0=x_banks[t, k][:].rearrange("p (b m) -> p m b", b=PACK),
                    scalar=neg_mean[t][:, 0:1],
                    in1=gamma_rows[:, cells].rearrange("p (m b) -> p m b", b=PACK),
                    op0=ALU.add,
                    op1=ALU.mult,
                )

        def store_rows(t):
            result = row_pool.tile([P, CELLS], F32, name="result")
            nc.vector.scalar_tensor_tensor(
                out=result[:],
                in0=centred[t][:],
                scalar=rstd[t][:, 0:1],
                in1=beta_rows[:],
                op0=ALU.mult,
                op1=ALU.add,
            )
            nc.sync.dma_start(out=out_rows[:, t, :], in_=result[:])

        for jb in range(PAIR_BLOCKS):
            second_product(0, jb)
            scale_drive(0, jb)
        for g in (1, 2, 0):
            quantise_cat(g, 1)
        partner_gain(0, 0)
        for c in range(N_COLS):
            products(0, c)
        for c in range(0, N_COLS, 2):
            sigmoids(1, c)
            sigmoids(1, c + 1)
            self_gain(1, c)
            self_gain(1, c + 1)
        for unit in units[1]:
            first_product(*unit)
            add_b1(*unit)
            if unit[1] == ROW_TILES - 1:
                quantise_h(unit[0], 1)
        for jb in range(PAIR_BLOCKS):
            second_product(1, jb)
            scale_drive(1, jb)

        def row_mean(t):
            row_layout(t)
            for k in range(2):
                sum_row(t, k)
            make_neg_mean(t)

        def row_rstd(t):
            for k in range(2):
                sum_squares(t, k)
            make_part_eps(t)
            make_rstd(t)

        row_mean(0)
        partner_gain(1, 0)
        for t in range(ROW_TILES):
            if t < TILES_PER_HALF:
                products(1, 2 * t)
                products(1, 2 * t + 1)
            if t + 1 < ROW_TILES:
                row_mean(t + 1)
            row_rstd(t)
            centre(t)
            if t > 0:
                store_rows(t - 1)
        store_rows(ROW_TILES - 1)
